import numpy as np
import ml_dtypes


def mxq(x, axis, fmt="e4m3"):
    dtype, down = {"e4m3": (ml_dtypes.float8_e4m3fn, 7), "e5m2": (ml_dtypes.float8_e5m2, 14)}[fmt]
    v = np.moveaxis(np.asarray(x, np.float32).astype(ml_dtypes.bfloat16).astype(np.float64), axis, -1)
    blocks = v.reshape(v.shape[:-1] + (-1, 32))
    amax = np.abs(blocks).max(-1, keepdims=True)
    byte = np.maximum(np.where(amax > 0, np.frexp(amax)[1] - 1 + 127, 0) - down, 1)
    scale = np.exp2(byte - 127.0)
    codes = (blocks / scale).astype(np.float32).astype(dtype).astype(np.float64)
    return np.moveaxis((codes * scale).reshape(v.shape), -1, axis)


WIDE = False


def mx_kscale(k):
    if not WIDE:
        return np.ones(k)
    levels = np.array([10, -10, 5, -5, 0])
    if k % 512:
        return np.exp2(np.random.permutation(np.resize(levels, k // 32))).repeat(32)
    a = np.empty((k // 512, 16))
    for p in range(k // 512):
        a[p, :8] = np.random.permutation(np.resize(levels, 8))
        for g in range(8):
            far = levels[np.abs(levels - a[p, g]) >= 10]
            a[p, g + 8] = far[np.random.randint(len(far))]
    return np.exp2(a.ravel()).repeat(32)


BF16 = ml_dtypes.bfloat16


def bf(x):
    return np.asarray(x, np.float32).astype(BF16)


def f64(x):
    return np.asarray(x).astype(np.float64)


T, M, D, A, BL, W = 1024, 1024, 1024, 250, 512, 1024


def draw0():
    s = mx_kscale(D)
    g = np.exp2(np.random.uniform(-1.0, 1.0, T))
    return {"q": bf(np.random.standard_normal((T, D)) * (3.0 / np.sqrt(D)) * g[:, None] * s),
            "k": bf(np.random.standard_normal((T, D)) * 0.5 / s)}


def core(q, k):
    logits = mxq(f64(q), 1, "e4m3") @ mxq(f64(k), 1, "e4m3").T
    sh = logits - logits.max(-1, keepdims=True)
    lp = sh - np.log(np.exp(sh).sum(-1, keepdims=True))
    entropy = -(np.exp(lp) * lp).sum(-1) / np.log(T)
    dist = np.abs(np.arange(T)[:, None] - np.arange(T)[None, :])
    mask = (dist >= A) | (dist == 0)
    ml = np.where(mask, -np.inf, logits)
    e = np.exp(ml - ml.max(-1, keepdims=True))
    att = e / e.sum(-1, keepdims=True)
    div_h = np.prod(1.0 - att, axis=1)
    div = div_h / np.sum(np.abs(div_h))
    return att, entropy, div


def e4m3fn_bytes(y):
    return np.clip(np.asarray(y, np.float64), -448.0, 448.0).astype(np.float32).astype(ml_dtypes.float8_e4m3fn).view(np.uint8)


def e4m3fn_values(b):
    return np.asarray(b, np.uint8).view(ml_dtypes.float8_e4m3fn).astype(np.float64)


def setup_inputs():
    d = draw0()
    x0 = np.asarray(d['q']).astype(np.float64)
    s = (np.max(np.abs(x0), axis=(0,), keepdims=True) / 448.0).astype(np.float32)
    out = {}
    for k, v in d.items():
        if k == 'q':
            out['q_bytes'] = e4m3fn_bytes(x0 / s.astype(np.float64))
            out['q_scale'] = s
        else:
            out[k] = v
    return out


def reference(q_bytes, q_scale, k):
    return core(e4m3fn_values(q_bytes) * q_scale.astype(np.float64), k)

@@ -1,0 +1,375 @@
+import math
+from contextlib import ExitStack
+
+import concourse.mybir as mybir
+from concourse.masks import make_identity
+
+FLOPS = 2 * 1024 * 1024 * 1024
+
+F32 = mybir.dt.float32
+BF16 = mybir.dt.bfloat16
+U32 = mybir.dt.uint32
+U8 = mybir.dt.uint8
+FP8 = mybir.dt.float8_e4m3fn
+FP8X4 = mybir.dt.float8_e4m3fn_x4
+ALU = mybir.AluOpType
+ACT = mybir.ActivationFunctionType
+AX = mybir.AxisListType
+
+P = 128
+T = 1024
+D = 1024
+NB = T // P
+BAND = 250
+WIN = 640
+NEG = -(2.0 ** 100)
+
+
+def tile_selfattention_pa_kernel(tc, q_bytes, q_scale, k, out_0, out_1, out_2):
+    nc = tc.nc
+    with ExitStack() as ctx:
+        const = ctx.enter_context(tc.tile_pool(name="const", bufs=1))
+        stage = ctx.enter_context(tc.tile_pool(name="stage", bufs=4))
+        work = ctx.enter_context(tc.tile_pool(name="work", bufs=4))
+        small = ctx.enter_context(tc.tile_pool(name="small", bufs=4))
+        psum = ctx.enter_context(tc.psum_pool(name="psum", bufs=8))
+
+        sc_b = const.tile([P, D], F32, name="sc_b")
+        sc_row = q_scale.rearrange("o k -> (o k)")
+        qbytes = []
+        kraw = []
+        for i in range(4):
+            qb = const.tile([P, 2, D], U8, name="qbytes%d" % i)
+            qbytes.append(qb)
+        nc.sync.dma_start(out=sc_b[:, 0:256], in_=sc_row[0:256].partition_broadcast(P))
+        nc.sync.dma_start(out=qbytes[0][:, 0, :], in_=q_bytes[0:P, :])
+        for c in range(1, 4):
+            nc.sync.dma_start(
+                out=sc_b[:, 256 * c : 256 * (c + 1)], in_=sc_row[256 * c : 256 * (c + 1)].partition_broadcast(P)
+            )
+        nc.sync.dma_start(out=qbytes[0][:, 1, :], in_=q_bytes[P : 2 * P, :])
+        for i in range(4):
+            if i > 0:
+                nc.sync.dma_start(
+                    out=qbytes[i][:], in_=q_bytes[256 * i : 256 * (i + 1), :].rearrange("(b p) k -> p b k", p=P)
+                )
+            for j in range(2):
+                kr = const.tile([P, D], BF16, name="kraw%d" % (2 * i + j))
+                nc.sync.dma_start(out=kr[:], in_=k[P * (2 * i + j) : P * (2 * i + j + 1), :])
+                kraw.append(kr)
+
+        warm = const.tile([P, 1], F32, name="warm")
+        warm2 = const.tile([P, 1], F32, name="warm2")
+        nc.vector.memset(warm[:], 0.0)
+        nc.scalar.activation(out=warm2[:], in_=warm[:], func=ACT.Exp)
+
+        ident = const.tile([P, P], F32, name="ident")
+        make_identity(nc, ident[:])
+        zeros = const.tile([P, WIN], F32, name="zeros")
+        mask = const.tile([P, WIN], F32, name="mask")
+        nc.vector.memset(mask[:], 0.0)
+        nc.vector.memset(zeros[:], 0.0)
+        nc.gpsimd.affine_select(
+            out=mask[:], in_=mask[:], pattern=[[1, WIN]], compare_op=ALU.is_ge, fill=NEG,
+            base=-(256 - BAND + 1), channel_multiplier=-1,
+        )
+        nc.gpsimd.affine_select(
+            out=mask[:], in_=mask[:], pattern=[[-1, WIN]], compare_op=ALU.is_ge, fill=NEG,
+            base=256 + BAND - 1, channel_multiplier=1,
+        )
+        nc.gpsimd.affine_select(
+            out=mask[:], in_=mask[:], pattern=[[1, WIN]], compare_op=ALU.not_equal, fill=NEG,
+            base=-256, channel_multiplier=-1,
+        )
+        ones = const.tile([P, P], F32, name="ones")
+        nc.vector.memset(ones[:], 1.0)
+        fin = const.tile([P, P], F32, name="fin")
+        nc.vector.memset(fin[:], 0.0)
+
+        z1 = const.tile([P, NB], F32, name="z1")
+        s1 = const.tile([P, NB], F32, name="s1")
+        nm1s = const.tile([P, NB], F32, name="nm1s")
+
+        kc = const.tile([P, 2, T], U32, name="kc", align_bytes=64)
+        ks = const.tile([P, 2, T], U8, name="ks", align_bytes=64)
+        gk = []
+        for h in range(2):
+            gkh = const.tile([P, 2, 2048], BF16, name="gk%d" % h, align_bytes=64)
+            gk.append(gkh)
+        qc = []
+        qs = []
+        for b in range(NB // 2):
+            qcb = const.tile([P, 512], U32, name="qc%d" % b, align_bytes=64)
+            qsb = const.tile([P, 512], U8, name="qs%d" % b, align_bytes=64)
+            qc.append(qcb)
+            qs.append(qsb)
+
+        def transposes(src):
+            words = src.bitcast(F32)
+            bank = psum.tile([P, 2, 2, P], F32, tag="bank", name="bank")
+            for g in range(2):
+                for u in range(2):
+                    nc.tensor.transpose(bank[:, g, u, :], words[:, 256 * g + u : 256 * (g + 1) : 2], ident[:])
+            return bank
+
+        qst = {}
+
+        def qm(b):
+            qbf = stage.tile([P, D], BF16, tag="qbf", name="qbf")
+            pieces = 4 if b == 0 else 1
+            cw = D // pieces
+            for c in range(pieces):
+                nc.vector.tensor_tensor(
+                    out=qbf[:, cw * c : cw * (c + 1)],
+                    in0=qbytes[b // 2][:, b % 2, cw * c : cw * (c + 1)].bitcast(FP8),
+                    in1=sc_b[:, cw * c : cw * (c + 1)],
+                    op=ALU.mult,
+                )
+            bank = transposes(qbf[:])
+            if b % 2 == 0:
+                gq = stage.tile([P, 2 * D], BF16, tag="gq", name="gq", align_bytes=64)
+                qst[b // 2] = gq
+            nc.scalar.copy(
+                out=qst[b // 2][:, D * (b % 2) : D * (b % 2 + 1)].bitcast(F32).rearrange(
+                    "p (g r u) -> p g r u", g=2, u=2
+                ),
+                in_=bank[:].rearrange("p g u r -> p g r u"),
+            )
+
+        def qq(pair):
+            nc.vector.quantize_mx(out=qc[pair][:].bitcast(FP8X4), scales=qs[pair][:], in_=qst[pair][:])
+
+        def k_front(b):
+            bank = transposes(kraw[b][:])
+            h, j = b // 4, b % 4
+            gw = gk[h][:].rearrange("p g c -> p (g c)").bitcast(F32).rearrange("p (g r u) -> p g r u", g=2, u=2)
+            nc.scalar.copy(out=gw[:, :, P * j : P * (j + 1), :], in_=bank[:].rearrange("p g u r -> p g r u"))
+
+        def k_quant(h):
+            for g in range(2):
+                nc.vector.quantize_mx(
+                    out=kc[:, g, 512 * h : 512 * (h + 1)].bitcast(FP8X4),
+                    scales=ks[:, g, 512 * h : 512 * (h + 1)],
+                    in_=gk[h][:, g, :],
+                )
+
+        def window(r):
+            return max(0, P * r - 256), min(T, P * r + 384)
+
+        for r in range(NB):
+            c0, c1 = window(r)
+            if c0 > 0:
+                nc.sync.dma_start(out=out_0[P * r : P * (r + 1), 0:c0], in_=zeros[:, 0:c0])
+            if c1 < T:
+                nc.sync.dma_start(out=out_0[P * r : P * (r + 1), c1:T], in_=zeros[:, 0 : T - c1])
+
+        logits = {}
+        st = {}
+
+        def mm(r):
+            banks = []
+            for h in range(2):
+                acc = psum.tile([P, 512], F32, tag="bank", name="acc")
+                for g in range(2):
+                    nc.tensor.matmul_mx(
+                        out=acc[:],
+                        lhsT=qc[r // 2][:, 256 * (r % 2) + P * g : 256 * (r % 2) + P * (g + 1)].bitcast(FP8X4),
+                        lhsT_scale=qs[r // 2][:, 256 * (r % 2) + P * g : 256 * (r % 2) + P * (g + 1)],
+                        rhs=kc[:, g, 512 * h : 512 * (h + 1)].bitcast(FP8X4),
+                        rhs_scale=ks[:, g, 512 * h : 512 * (h + 1)],
+                        start=(g == 0),
+                        stop=(g == 1),
+                    )
+                banks.append(acc)
+            logits[r] = banks
+
+        def pieces_of(r):
+            c0, c1 = window(r)
+            out = []
+            for h in range(2):
+                lo, hi = max(c0, 512 * h), min(c1, 512 * (h + 1))
+                if lo < hi:
+                    out.append((h, lo, hi))
+            return out
+
+        def a1(r):
+            nl = work.tile([P, T], F32, tag="nl", name="nl")
+            t0 = small.tile([P, 1], F32, tag="t0", name="t0")
+            nc.vector.tensor_scalar(
+                out=nl[:, 0:512], in0=logits[r][0][:], scalar1=-1.0, scalar2=None,
+                op0=ALU.mult, op1=ALU.min, accum_out=t0[:],
+            )
+            ml = work.tile([P, WIN], F32, tag="ml", name="ml")
+            st[r] = {"nl": nl, "t0": t0, "ml": ml}
+
+        def a2(r):
+            nc.vector.tensor_scalar(
+                out=st[r]["nl"][:, 512:T], in0=logits[r][1][:], scalar1=-1.0, scalar2=st[r]["t0"][:],
+                op0=ALU.mult, op1=ALU.min, accum_out=nm1s[:, r : r + 1],
+            )
+
+        def bmask(r, n):
+            c0, c1 = window(r)
+            mo = c0 - (P * r - 256)
+            h, lo, hi = pieces_of(r)[n]
+            nc.vector.tensor_tensor(
+                out=st[r]["ml"][:, lo - c0 : hi - c0],
+                in0=logits[r][h][:, lo - 512 * h : hi - 512 * h],
+                in1=mask[:, lo - c0 + mo : hi - c0 + mo],
+                op=ALU.add,
+            )
+
+        def cmax(r):
+            c0, c1 = window(r)
+            nm2 = small.tile([P, 1], F32, tag="nm2", name="nm2")
+            nc.vector.tensor_reduce(out=nm2[:], in_=st[r]["ml"][:, 0 : c1 - c0], axis=AX.X, op=ALU.max, negate=True)
+            st[r]["nm2"] = nm2
+
+        def exp1(r):
+            e1 = work.tile([P, T], F32, tag="e1", name="e1")
+            nc.scalar.activation(
+                out=e1[:], in_=st[r]["nl"][:], func=ACT.Exp, bias=nm1s[:, r : r + 1], scale=-1.0,
+                accum_out=z1[:, r : r + 1],
+            )
+            st[r]["e1"] = e1
+
+        def exp2(r):
+            c0, c1 = window(r)
+            w = c1 - c0
+            e2 = work.tile([P, WIN], F32, tag="e2", name="e2")
+            z2 = small.tile([P, 1], F32, tag="z2", name="z2")
+            nc.scalar.activation(
+                out=e2[:, 0:w], in_=st[r]["ml"][:, 0:w], func=ACT.Exp, bias=st[r]["nm2"][:], scale=1.0, accum_out=z2[:]
+            )
+            st[r]["e2"] = e2
+            st[r]["z2"] = z2
+
+        def rcp(r):
+            rz2 = small.tile([P, 1], F32, tag="rz2", name="rz2")
+            nc.vector.reciprocal(out=rz2[:], in_=st[r]["z2"][:])
+            st[r]["rz2"] = rz2
+
+        def norm(r, on_vector):
+            c0, c1 = window(r)
+            w = c1 - c0
+            att = work.tile([P, WIN], F32, tag="att", name="att")
+            if on_vector:
+                nc.vector.tensor_scalar(
+                    out=att[:, 0:w], in0=st[r]["e2"][:, 0:w], scalar1=st[r]["rz2"][:], scalar2=None, op0=ALU.mult
+                )
+            else:
+                nc.gpsimd.tensor_scalar(
+                    out=att[:, 0:w], in0=st[r]["e2"][:, 0:w], scalar1=st[r]["rz2"][:], scalar2=0.0,
+                    op0=ALU.mult, op1=ALU.add,
+                )
+            nc.sync.dma_start(out=out_0[P * r : P * (r + 1), c0:c1], in_=att[:, 0:w])
+            st[r]["att"] = att
+
+        def prod_el(r):
+            pr = work.tile([P, T], F32, tag="pr", name="pr")
+            nc.gpsimd.tensor_tensor(out=pr[:], in0=st[r]["e1"][:], in1=st[r]["nl"][:], op=ALU.mult)
+            st[r]["pr"] = pr
+
+        def sum_el(r):
+            junk = work.tile([P, T], F32, tag="junk", name="junk")
+            nc.scalar.activation(out=junk[:], in_=st[r]["pr"][:], func=ACT.Copy, accum_out=s1[:, r : r + 1])
+
+        def prod_sum_vector(r):
+            pr = work.tile([P, T], F32, tag="pr", name="pr")
+            nc.vector.scalar_tensor_tensor(
+                out=pr[:], in0=st[r]["nl"][:], scalar=1.0, in1=st[r]["e1"][:], op0=ALU.mult, op1=ALU.mult,
+                accum_out=s1[:, r : r + 1],
+            )
+
+        def pdiv(r):
+            c0, c1 = window(r)
+            w = c1 - c0
+            junk2 = work.tile([P, WIN], F32, tag="junk2", name="junk2")
+            nc.vector.tensor_scalar(
+                out=junk2[:, 0:w], in0=st[r]["att"][:, 0:w], scalar1=1.0, scalar2=None,
+                op0=ALU.subtract, op1=ALU.mult, accum_out=fin[:, r : r + 1],
+            )
+
+        def finish():
+            rz1 = small.tile([P, NB], F32, tag="rz1", name="rz1")
+            nc.vector.reciprocal(out=rz1[:], in_=z1[:])
+            lnz = small.tile([P, NB], F32, tag="lnz", name="lnz")
+            nc.scalar.activation(out=lnz[:], in_=z1[:], func=ACT.Ln)
+            mean = small.tile([P, NB], F32, tag="mean", name="mean")
+            nc.vector.tensor_tensor(out=mean[:], in0=s1[:], in1=rz1[:], op=ALU.mult)
+            dsum = small.tile([P, 1], F32, tag="dsum", name="dsum")
+            nc.vector.tensor_reduce(out=dsum[:], in_=fin[:, 0:NB], axis=AX.X, op=ALU.add, apply_absolute_value=True)
+            tot = psum.tile([P, 512], F32, tag="bank", name="tot")
+            nc.tensor.matmul(tot[:, 0:1], lhsT=ones[:], rhs=dsum[:], start=True, stop=True)
+            shifted = small.tile([P, NB], F32, tag="shifted", name="shifted")
+            nc.vector.tensor_tensor(out=shifted[:], in0=mean[:], in1=nm1s[:], op=ALU.subtract)
+            nc.vector.tensor_tensor(out=fin[:, 32 : 32 + NB], in0=lnz[:], in1=shifted[:], op=ALU.add)
+            rtot = small.tile([P, 1], F32, tag="rtot", name="rtot")
+            nc.vector.reciprocal(out=rtot[:], in_=tot[:, 0:1])
+            turned = psum.tile([P, 512], F32, tag="bank", name="turned")
+            nc.tensor.transpose(turned[:, 0:P], fin[:], ident[:])
+            res = const.tile([P, P], F32, name="res")
+            nc.vector.tensor_scalar(
+                out=res[0:NB, :], in0=turned[0:NB, 0:P], scalar1=rtot[0:NB, :], scalar2=None, op0=ALU.mult
+            )
+            nc.scalar.activation(
+                out=res[32 : 32 + NB, :], in_=turned[32 : 32 + NB, 0:P], func=ACT.Copy,
+                scale=1.0 / math.log(float(T)),
+            )
+            nc.sync.dma_start(out=out_2.rearrange("(r p) -> r p", p=P), in_=res[0:NB, :])
+            nc.sync.dma_start(out=out_1.rearrange("(r p) -> r p", p=P), in_=res[32 : 32 + NB, :])
+
+        with tc.manual_schedule(engines={mybir.EngineType.DVE}):
+            qm(0)
+            qm(1)
+            k_front(0)
+            k_front(1)
+            qm(2)
+            k_front(2)
+            k_front(3)
+            qm(3)
+            qq(0)
+            qm(4)
+            k_front(4)
+            k_front(5)
+            qm(5)
+            qq(1)
+            k_quant(0)
+            k_front(6)
+            k_front(7)
+            qm(6)
+            k_quant(1)
+            qq(2)
+            mm(0)
+            qm(7)
+            mm(1)
+        last = NB - 1
+        with tc.manual_schedule():
+            for i in range(NB + 3):
+                if 2 <= i + 1 < NB:
+                    mm(i + 1)
+                if 0 <= i - 1 < NB:
+                    exp2(i - 1)
+                if 0 <= i - 2 < last:
+                    prod_el(i - 2)
+                    norm(i - 2, False)
+                if i < NB:
+                    a1(i)
+                    for n in range(len(pieces_of(i))):
+                        bmask(i, n)
+                if 0 <= i - 2 < last:
+                    sum_el(i - 2)
+                if i < NB:
+                    a2(i)
+                    exp1(i)
+                    cmax(i)
+                if i == 0:
+                    qq(3)
+                if 0 <= i - 3 < NB:
+                    pdiv(i - 3)
+                if 0 <= i - 1 < NB:
+                    rcp(i - 1)
+                if i - 1 == last:
+                    prod_sum_vector(last)
+                    norm(last, True)
+            finish()

@@ -23,6 +23,7 @@ NB = T // P
 BAND = 250
 WIN = 640
 NEG = -(2.0 ** 100)
+NFOLD = 6
 
 
 def tile_selfattention_pa_kernel(tc, q_bytes, q_scale, k, out_0, out_1, out_2):
@@ -257,6 +258,8 @@ def tile_selfattention_pa_kernel(tc, q_bytes, q_scale, k, out_0, out_1, out_2):
                 nc.vector.tensor_scalar(
                     out=att[:, 0:w], in0=st[r]["e2"][:, 0:w], scalar1=st[r]["rz2"][:], scalar2=None, op0=ALU.mult
                 )
+            elif w == WIN:
+                nc.scalar.activation(out=att[:, 0:w], in_=st[r]["e2"][:, 0:w], func=ACT.Copy, scale=st[r]["rz2"][:])
             else:
                 nc.gpsimd.tensor_scalar(
                     out=att[:, 0:w], in0=st[r]["e2"][:, 0:w], scalar1=st[r]["rz2"][:], scalar2=0.0,
@@ -269,6 +272,18 @@ def tile_selfattention_pa_kernel(tc, q_bytes, q_scale, k, out_0, out_1, out_2):
             pr = work.tile([P, T], F32, tag="pr", name="pr")
             nc.gpsimd.tensor_tensor(out=pr[:], in0=st[r]["e1"][:], in1=st[r]["nl"][:], op=ALU.mult)
             st[r]["pr"] = pr
+
+        def fold(r):
+            acc = psum.tile([P, 512], F32, tag="bank", name="fold")
+            for b in range(NB):
+                nc.tensor.matmul(
+                    acc[:, 0:P], lhsT=ident[:], rhs=st[r]["pr"][:, P * b : P * (b + 1)], start=(b == 0), stop=(b == NB - 1)
+                )
+            st[r]["fold"] = acc
+
+        def sum_fold(r):
+            junk = work.tile([P, T], F32, tag="junk", name="junk")
+            nc.scalar.activation(out=junk[:, 0:P], in_=st[r]["fold"][:, 0:P], func=ACT.Copy, accum_out=s1[:, r : r + 1])
 
         def sum_el(r):
             junk = work.tile([P, T], F32, tag="junk", name="junk")
@@ -290,11 +305,14 @@ def tile_selfattention_pa_kernel(tc, q_bytes, q_scale, k, out_0, out_1, out_2):
                 op0=ALU.subtract, op1=ALU.mult, accum_out=fin[:, r : r + 1],
             )
 
+        lnz = const.tile([P, NB], F32, name="lnz")
+
+        def log_z():
+            nc.scalar.activation(out=lnz[:], in_=z1[:], func=ACT.Ln)
+
         def finish():
             rz1 = small.tile([P, NB], F32, tag="rz1", name="rz1")
             nc.vector.reciprocal(out=rz1[:], in_=z1[:])
-            lnz = small.tile([P, NB], F32, tag="lnz", name="lnz")
-            nc.scalar.activation(out=lnz[:], in_=z1[:], func=ACT.Ln)
             mean = small.tile([P, NB], F32, tag="mean", name="mean")
             nc.vector.tensor_tensor(out=mean[:], in0=s1[:], in1=rz1[:], op=ALU.mult)
             dsum = small.tile([P, 1], F32, tag="dsum", name="dsum")
@@ -348,8 +366,12 @@ def tile_selfattention_pa_kernel(tc, q_bytes, q_scale, k, out_0, out_1, out_2):
             for i in range(NB + 3):
                 if 2 <= i + 1 < NB:
                     mm(i + 1)
+                if 0 <= i - 3 < NFOLD:
+                    fold(i - 3)
                 if 0 <= i - 1 < NB:
                     exp2(i - 1)
+                if i - 1 == last:
+                    log_z()
                 if 0 <= i - 2 < last:
                     prod_el(i - 2)
                     norm(i - 2, False)
@@ -357,7 +379,9 @@ def tile_selfattention_pa_kernel(tc, q_bytes, q_scale, k, out_0, out_1, out_2):
                     a1(i)
                     for n in range(len(pieces_of(i))):
                         bmask(i, n)
-                if 0 <= i - 2 < last:
+                if 0 <= i - 3 < NFOLD:
+                    sum_fold(i - 3)
+                if NFOLD <= i - 2 < last:
                     sum_el(i - 2)
                 if i < NB:
                     a2(i)
@@ -367,9 +391,10 @@ def tile_selfattention_pa_kernel(tc, q_bytes, q_scale, k, out_0, out_1, out_2):
                     qq(3)
                 if 0 <= i - 3 < NB:
                     pdiv(i - 3)
+                if i - 1 == last:
+                    prod_sum_vector(last)
                 if 0 <= i - 1 < NB:
                     rcp(i - 1)
                 if i - 1 == last:
-                    prod_sum_vector(last)
                     norm(last, True)
             finish()

@@ -45,7 +45,7 @@ def tile_selfattention_pa_kernel(tc, q_bytes, q_scale, k, out_0, out_1, out_2):
         nc.sync.dma_start(out=sc_b[:, 0:256], in_=sc_row[0:256].partition_broadcast(P))
         nc.sync.dma_start(out=qbytes[0][:, 0, :], in_=q_bytes[0:P, :])
         for c in range(1, 4):
-            nc.sync.dma_start(
+            nc.scalar.dma_start(
                 out=sc_b[:, 256 * c : 256 * (c + 1)], in_=sc_row[256 * c : 256 * (c + 1)].partition_broadcast(P)
             )
         nc.sync.dma_start(out=qbytes[0][:, 1, :], in_=q_bytes[P : 2 * P, :])

@@ -157,7 +157,7 @@ def tile_selfattention_pa_kernel(tc, q_bytes, q_scale, k, out_0, out_1, out_2):
         def window(r):
             return max(0, P * r - 256), min(T, P * r + 384)
 
-        for r in range(NB):
+        def zero_fill(r):
             c0, c1 = window(r)
             if c0 > 0:
                 nc.sync.dma_start(out=out_0[P * r : P * (r + 1), 0:c0], in_=zeros[:, 0:c0])
@@ -375,6 +375,11 @@ def tile_selfattention_pa_kernel(tc, q_bytes, q_scale, k, out_0, out_1, out_2):
                 if 0 <= i - 2 < last:
                     prod_el(i - 2)
                     norm(i - 2, False)
+                if i == 2:
+                    zero_fill(0)
+                    zero_fill(1)
+                if 2 <= i < NB:
+                    zero_fill(i)
                 if i < NB:
                     a1(i)
                     for n in range(len(pieces_of(i))):

@@ -115,17 +115,27 @@ def tile_selfattention_pa_kernel(tc, q_bytes, q_scale, k, out_0, out_1, out_2):
 
         qst = {}
 
+        def widen(b, qbf, lo, hi):
+            nc.vector.tensor_tensor(
+                out=qbf[:, lo:hi], in0=qbytes[b // 2][:, b % 2, lo:hi].bitcast(FP8), in1=sc_b[:, lo:hi], op=ALU.mult
+            )
+
+        first = []
+
+        def widen_first():
+            for b in range(2):
+                qbf = stage.tile([P, D], BF16, tag="qbf", name="qbf")
+                first.append(qbf)
+            for c in range(4):
+                for b in range(2):
+                    widen(b, first[b], 256 * c, 256 * (c + 1))
+
         def qm(b):
             qbf = stage.tile([P, D], BF16, tag="qbf", name="qbf")
-            pieces = 4 if b == 0 else 1
-            cw = D // pieces
-            for c in range(pieces):
-                nc.vector.tensor_tensor(
-                    out=qbf[:, cw * c : cw * (c + 1)],
-                    in0=qbytes[b // 2][:, b % 2, cw * c : cw * (c + 1)].bitcast(FP8),
-                    in1=sc_b[:, cw * c : cw * (c + 1)],
-                    op=ALU.mult,
-                )
+            widen(b, qbf, 0, D)
+            q_turn(b, qbf)
+
+        def q_turn(b, qbf):
             bank = transposes(qbf[:])
             if b % 2 == 0:
                 gq = stage.tile([P, 2 * D], BF16, tag="gq", name="gq", align_bytes=64)
@@ -338,8 +348,9 @@ def tile_selfattention_pa_kernel(tc, q_bytes, q_scale, k, out_0, out_1, out_2):
             nc.sync.dma_start(out=out_1.rearrange("(r p) -> r p", p=P), in_=res[32 : 32 + NB, :])
 
         with tc.manual_schedule(engines={mybir.EngineType.DVE}):
-            qm(0)
-            qm(1)
+            widen_first()
+            q_turn(0, first[0])
+            q_turn(1, first[1])
             k_front(0)
             k_front(1)
             qm(2)

@@ -22,8 +22,10 @@ D = 1024
 NB = T // P
 BAND = 250
 WIN = 640
-NEG = -(2.0 ** 100)
-NFOLD = 6
+EDGE = 136
+BIG = 2.0 ** 100
+FOLDED = (1, 2, 3, 4)
+ON_POOL = 6
 
 
 def tile_selfattention_pa_kernel(tc, q_bytes, q_scale, k, out_0, out_1, out_2):
@@ -35,29 +37,44 @@ def tile_selfattention_pa_kernel(tc, q_bytes, q_scale, k, out_0, out_1, out_2):
         small = ctx.enter_context(tc.tile_pool(name="small", bufs=4))
         psum = ctx.enter_context(tc.psum_pool(name="psum", bufs=8))
 
-        sc_b = const.tile([P, D], F32, name="sc_b")
-        sc_row = q_scale.rearrange("o k -> (o k)")
+        def one_bank(name):
+            return psum.tile([P, 512], F32, tag="bank", name=name)
+
+        sct = const.tile([P, 2, 4], F32, name="sct")
         qbytes = []
         kraw = []
         for i in range(4):
             qb = const.tile([P, 2, D], U8, name="qbytes%d" % i)
             qbytes.append(qb)
-        nc.sync.dma_start(out=sc_b[:, 0:256], in_=sc_row[0:256].partition_broadcast(P))
-        nc.sync.dma_start(out=qbytes[0][:, 0, :], in_=q_bytes[0:P, :])
-        for c in range(1, 4):
-            nc.scalar.dma_start(
-                out=sc_b[:, 256 * c : 256 * (c + 1)], in_=sc_row[256 * c : 256 * (c + 1)].partition_broadcast(P)
+        for b in range(NB):
+            kr = const.tile([P, D], BF16, name="kraw%d" % b)
+            kraw.append(kr)
+
+        def load_q(b):
+            nc.sync.dma_start(out=qbytes[b // 2][:, b % 2, :], in_=q_bytes[P * b : P * (b + 1), :])
+
+        def load_q_pair(i):
+            nc.sync.dma_start(
+                out=qbytes[i][:], in_=q_bytes[256 * i : 256 * (i + 1), :].rearrange("(b p) k -> p b k", p=P)
             )
-        nc.sync.dma_start(out=qbytes[0][:, 1, :], in_=q_bytes[P : 2 * P, :])
-        for i in range(4):
-            if i > 0:
-                nc.sync.dma_start(
-                    out=qbytes[i][:], in_=q_bytes[256 * i : 256 * (i + 1), :].rearrange("(b p) k -> p b k", p=P)
-                )
-            for j in range(2):
-                kr = const.tile([P, D], BF16, name="kraw%d" % (2 * i + j))
-                nc.sync.dma_start(out=kr[:], in_=k[P * (2 * i + j) : P * (2 * i + j + 1), :])
-                kraw.append(kr)
+
+        def load_k(b):
+            nc.sync.dma_start(out=kraw[b][:], in_=k[P * b : P * (b + 1), :])
+
+        nc.scalar.dma_start(out=sct[:], in_=q_scale.rearrange("o (g p t) -> p (o g) t", p=P, t=4))
+        load_q(0)
+        load_q(1)
+        load_q_pair(1)
+        load_k(0)
+        load_k(1)
+        load_k(2)
+        load_k(3)
+        load_q_pair(2)
+        load_k(4)
+        load_k(5)
+        load_k(6)
+        load_k(7)
+        load_q_pair(3)
 
         warm = const.tile([P, 1], F32, name="warm")
         warm2 = const.tile([P, 1], F32, name="warm2")
@@ -67,20 +84,20 @@ def tile_selfattention_pa_kernel(tc, q_bytes, q_scale, k, out_0, out_1, out_2):
         ident = const.tile([P, P], F32, name="ident")
         make_identity(nc, ident[:])
         zeros = const.tile([P, WIN], F32, name="zeros")
-        mask = const.tile([P, WIN], F32, name="mask")
+        mask = const.tile([P, 2 * EDGE + P], F32, name="mask")
         nc.vector.memset(mask[:], 0.0)
         nc.vector.memset(zeros[:], 0.0)
         nc.gpsimd.affine_select(
-            out=mask[:], in_=mask[:], pattern=[[1, WIN]], compare_op=ALU.is_ge, fill=NEG,
+            out=mask[:, EDGE : 2 * EDGE], in_=mask[:, EDGE : 2 * EDGE], pattern=[[1, EDGE]], compare_op=ALU.is_ge, fill=BIG,
             base=-(256 - BAND + 1), channel_multiplier=-1,
         )
         nc.gpsimd.affine_select(
-            out=mask[:], in_=mask[:], pattern=[[-1, WIN]], compare_op=ALU.is_ge, fill=NEG,
-            base=256 + BAND - 1, channel_multiplier=1,
+            out=mask[:, 0:EDGE], in_=mask[:, 0:EDGE], pattern=[[-1, EDGE]], compare_op=ALU.is_ge, fill=BIG,
+            base=BAND - 1 - (WIN - 256 - EDGE), channel_multiplier=1,
         )
         nc.gpsimd.affine_select(
-            out=mask[:], in_=mask[:], pattern=[[1, WIN]], compare_op=ALU.not_equal, fill=NEG,
-            base=-256, channel_multiplier=-1,
+            out=mask[:, 2 * EDGE :], in_=mask[:, 2 * EDGE :], pattern=[[1, P]], compare_op=ALU.not_equal, fill=BIG,
+            base=0, channel_multiplier=-1,
         )
         ones = const.tile([P, P], F32, name="ones")
         nc.vector.memset(ones[:], 1.0)
@@ -93,10 +110,11 @@ def tile_selfattention_pa_kernel(tc, q_bytes, q_scale, k, out_0, out_1, out_2):
 
         kc = const.tile([P, 2, T], U32, name="kc", align_bytes=64)
         ks = const.tile([P, 2, T], U8, name="ks", align_bytes=64)
-        gk = []
-        for h in range(2):
-            gkh = const.tile([P, 2, 2048], BF16, name="gk%d" % h, align_bytes=64)
-            gk.append(gkh)
+        KGROUPS = ((0, 4), (4, 2), (6, 2))
+        gk = {}
+        for b0, n in KGROUPS:
+            gkb = const.tile([P, 2, 512 * n], BF16, name="gk%d" % b0, align_bytes=64)
+            gk[b0] = gkb
         qc = []
         qs = []
         for b in range(NB // 2):
@@ -105,63 +123,86 @@ def tile_selfattention_pa_kernel(tc, q_bytes, q_scale, k, out_0, out_1, out_2):
             qc.append(qcb)
             qs.append(qsb)
 
-        def transposes(src):
+        def transposes(src, bank):
             words = src.bitcast(F32)
-            bank = psum.tile([P, 2, 2, P], F32, tag="bank", name="bank")
             for g in range(2):
                 for u in range(2):
-                    nc.tensor.transpose(bank[:, g, u, :], words[:, 256 * g + u : 256 * (g + 1) : 2], ident[:])
-            return bank
+                    nc.tensor.transpose(
+                        bank[:, P * (2 * g + u) : P * (2 * g + u + 1)], words[:, 256 * g + u : 256 * (g + 1) : 2], ident[:]
+                    )
 
-        qst = {}
+        gq = []
+        for i in range(NB // 2):
+            g_pair = const.tile([P, 2 * D], BF16, name="gq%d" % i, align_bytes=64)
+            gq.append(g_pair)
+        qbf = {}
+        qbank = {}
+        kbank = {}
+        graw = {}
 
-        def widen(b, qbf, lo, hi):
-            nc.vector.tensor_tensor(
-                out=qbf[:, lo:hi], in0=qbytes[b // 2][:, b % 2, lo:hi].bitcast(FP8), in1=sc_b[:, lo:hi], op=ALU.mult
-            )
+        def cast(b, engine):
+            t = stage.tile([P, D], BF16, tag="qbf", name="qbf")
+            src = qbytes[b // 2][:, b % 2, :].bitcast(FP8)
+            if engine is nc.scalar:
+                nc.scalar.copy(out=t[:], in_=src)
+            else:
+                engine.tensor_copy(out=t[:], in_=src)
+            qbf[b] = t
 
-        first = []
+        def turn(b):
+            bank = one_bank("turn")
+            transposes(qbf[b][:], bank)
+            qbank[b] = bank
 
-        def widen_first():
-            for b in range(2):
-                qbf = stage.tile([P, D], BF16, tag="qbf", name="qbf")
-                first.append(qbf)
-            for c in range(4):
-                for b in range(2):
-                    widen(b, first[b], 256 * c, 256 * (c + 1))
+        def scale_out(b):
+            for g in range(2):
+                lo = D * (b % 2) + 512 * g
+                nc.vector.tensor_tensor(
+                    out=gq[b // 2][:, lo : lo + 512].rearrange("p (r u e) -> p r u e", u=2, e=2),
+                    in0=qbank[b][:, 256 * g : 256 * (g + 1)].bitcast(BF16).rearrange("p (u r e) -> p r u e", u=2, e=2),
+                    in1=sct[:, g, :].rearrange("p (u e) -> p u e", u=2).unsqueeze(1).to_broadcast([P, P, 2, 2]),
+                    op=ALU.mult,
+                )
 
-        def qm(b):
-            qbf = stage.tile([P, D], BF16, tag="qbf", name="qbf")
-            widen(b, qbf, 0, D)
-            q_turn(b, qbf)
-
-        def q_turn(b, qbf):
-            bank = transposes(qbf[:])
-            if b % 2 == 0:
-                gq = stage.tile([P, 2 * D], BF16, tag="gq", name="gq", align_bytes=64)
-                qst[b // 2] = gq
+        def copy_out(b):
+            t = stage.tile([P, D], BF16, tag="graw", name="graw")
             nc.scalar.copy(
-                out=qst[b // 2][:, D * (b % 2) : D * (b % 2 + 1)].bitcast(F32).rearrange(
-                    "p (g r u) -> p g r u", g=2, u=2
-                ),
-                in_=bank[:].rearrange("p g u r -> p g r u"),
+                out=t[:].bitcast(F32).rearrange("p (g r u) -> p g r u", g=2, u=2),
+                in_=qbank[b][:].rearrange("p (g u r) -> p g r u", g=2, u=2),
+            )
+            graw[b] = t
+
+        def scale_pool(b):
+            lo = D * (b % 2)
+            nc.gpsimd.tensor_tensor(
+                out=gq[b // 2][:, lo : lo + D].rearrange("p (g r t) -> p g r t", g=2, t=4),
+                in0=graw[b][:].rearrange("p (g r t) -> p g r t", g=2, t=4),
+                in1=sct[:].unsqueeze(2).to_broadcast([P, 2, P, 4]),
+                op=ALU.mult,
             )
 
         def qq(pair):
-            nc.vector.quantize_mx(out=qc[pair][:].bitcast(FP8X4), scales=qs[pair][:], in_=qst[pair][:])
+            nc.vector.quantize_mx(out=qc[pair][:].bitcast(FP8X4), scales=qs[pair][:], in_=gq[pair][:])
 
-        def k_front(b):
-            bank = transposes(kraw[b][:])
-            h, j = b // 4, b % 4
-            gw = gk[h][:].rearrange("p g c -> p (g c)").bitcast(F32).rearrange("p (g r u) -> p g r u", g=2, u=2)
-            nc.scalar.copy(out=gw[:, :, P * j : P * (j + 1), :], in_=bank[:].rearrange("p g u r -> p g r u"))
+        def k_turn(b):
+            kbank[b] = one_bank("kturn")
+            transposes(kraw[b][:], kbank[b])
 
-        def k_quant(h):
+        def k_copy(b):
+            bank = kbank[b]
+            b0 = max(x for x, n in KGROUPS if x <= b)
+            j = b - b0
+            gw = gk[b0][:].rearrange("p g c -> p (g c)").bitcast(F32).rearrange("p (g r u) -> p g r u", g=2, u=2)
+            nc.scalar.copy(
+                out=gw[:, :, P * j : P * (j + 1), :], in_=bank[:].rearrange("p (g u r) -> p g r u", g=2, u=2)
+            )
+
+        def k_quant(b, n):
             for g in range(2):
                 nc.vector.quantize_mx(
-                    out=kc[:, g, 512 * h : 512 * (h + 1)].bitcast(FP8X4),
-                    scales=ks[:, g, 512 * h : 512 * (h + 1)],
-                    in_=gk[h][:, g, :],
+                    out=kc[:, g, P * b : P * (b + n)].bitcast(FP8X4),
+                    scales=ks[:, g, P * b : P * (b + n)],
+                    in_=gk[b][:, g, :],
                 )
 
         def window(r):
@@ -174,83 +215,160 @@ def tile_selfattention_pa_kernel(tc, q_bytes, q_scale, k, out_0, out_1, out_2):
             if c1 < T:
                 nc.sync.dma_start(out=out_0[P * r : P * (r + 1), c1:T], in_=zeros[:, 0 : T - c1])
 
+        CORE = P - (EDGE - P)
+
+        def layout(r):
+            want = [r + 1, r + 2, r - 2, r - 1]
+            far = [x for x in range(NB) if x != r and x not in want]
+            first = []
+            for x in want:
+                first.append(x if 0 <= x < NB else far.pop(0))
+            lay = {"banks": [first, [r] + far]}
+            base = P * r - 256
+            right = WIN - EDGE
+            edges = []
+            if r + 1 < NB:
+                edges.append((CORE, 0, base + right, EDGE if r + 2 < NB else EDGE - P))
+            if r > 0:
+                if r > 1:
+                    edges.append((256, EDGE, base, EDGE))
+                else:
+                    edges.append((384, EDGE + P, 0, EDGE - P))
+            lay["edges"] = edges
+            core = []
+            if r > 0:
+                core.append((512 - CORE, base + EDGE))
+            if r + 1 < NB:
+                core.append((0, P * (r + 1)))
+            lay["core"] = core
+            lay["rest"] = (CORE if r + 1 < NB else 0, 512 - CORE if r > 0 else 512)
+            return lay
+
+        lays = [layout(r) for r in range(NB)]
         logits = {}
         st = {}
 
-        def mm(r):
-            banks = []
-            for h in range(2):
-                acc = psum.tile([P, 512], F32, tag="bank", name="acc")
-                for g in range(2):
-                    nc.tensor.matmul_mx(
-                        out=acc[:],
-                        lhsT=qc[r // 2][:, 256 * (r % 2) + P * g : 256 * (r % 2) + P * (g + 1)].bitcast(FP8X4),
-                        lhsT_scale=qs[r // 2][:, 256 * (r % 2) + P * g : 256 * (r % 2) + P * (g + 1)],
-                        rhs=kc[:, g, 512 * h : 512 * (h + 1)].bitcast(FP8X4),
-                        rhs_scale=ks[:, g, 512 * h : 512 * (h + 1)],
-                        start=(g == 0),
-                        stop=(g == 1),
-                    )
-                banks.append(acc)
-            logits[r] = banks
-
-        def pieces_of(r):
-            c0, c1 = window(r)
+        def runs_of(blocks):
             out = []
-            for h in range(2):
-                lo, hi = max(c0, 512 * h), min(c1, 512 * (h + 1))
-                if lo < hi:
-                    out.append((h, lo, hi))
+            place = 0
+            while place < len(blocks):
+                n = 1
+                while place + n < len(blocks) and blocks[place + n] == blocks[place] + n:
+                    n += 1
+                if n == 3:
+                    n = 2
+                out.append((place, blocks[place], n))
+                place += n
             return out
 
-        def a1(r):
-            nl = work.tile([P, T], F32, tag="nl", name="nl")
-            t0 = small.tile([P, 1], F32, tag="t0", name="t0")
-            nc.vector.tensor_scalar(
-                out=nl[:, 0:512], in0=logits[r][0][:], scalar1=-1.0, scalar2=None,
-                op0=ALU.mult, op1=ALU.min, accum_out=t0[:],
-            )
-            ml = work.tile([P, WIN], F32, tag="ml", name="ml")
-            st[r] = {"nl": nl, "t0": t0, "ml": ml}
+        def mm(r):
+            logits[r] = []
+            for h in range(2):
+                acc = one_bank("acc")
+                for place, blk, n in runs_of(lays[r]["banks"][h]):
+                    for g in range(2):
+                        nc.tensor.matmul_mx(
+                            out=acc[:, P * place : P * (place + n)],
+                            lhsT=qc[r // 2][:, 256 * (r % 2) + P * g : 256 * (r % 2) + P * (g + 1)].bitcast(FP8X4),
+                            lhsT_scale=qs[r // 2][:, 256 * (r % 2) + P * g : 256 * (r % 2) + P * (g + 1)],
+                            rhs=kc[:, g, P * blk : P * (blk + n)].bitcast(FP8X4),
+                            rhs_scale=ks[:, g, P * blk : P * (blk + n)],
+                            start=(g == 0),
+                            stop=(g == 1),
+                        )
+                logits[r].append(acc)
 
-        def a2(r):
+        def width_masked(r):
+            return P + sum(e[3] for e in lays[r]["edges"])
+
+        def width_core(r):
+            return CORE * len(lays[r]["core"])
+
+        def a_core(r, c):
+            if c == 0:
+                work_w = work.tile([P, 400 + T], F32, tag="w", name="w")
+                st[r] = {"w": work_w, "tb": None}
+            if c >= len(lays[r]["core"]):
+                return
+            m = width_masked(r)
+            tb = st[r]["tb"]
+            t_new = small.tile([P, 1], F32, tag="tb%d" % c, name="tb")
+            s = lays[r]["core"][c][0]
             nc.vector.tensor_scalar(
-                out=st[r]["nl"][:, 512:T], in0=logits[r][1][:], scalar1=-1.0, scalar2=st[r]["t0"][:],
+                out=st[r]["w"][:, m + CORE * c : m + CORE * (c + 1)], in0=logits[r][0][:, s : s + CORE], scalar1=-1.0,
+                scalar2=None if tb is None else tb[:], op0=ALU.mult, op1=ALU.min, accum_out=t_new[:],
+            )
+            st[r]["tb"] = t_new
+
+        def a_rest(r):
+            t1 = small.tile([P, 1], F32, tag="t1", name="t1")
+            st[r]["t1"] = t1
+            lo, hi = lays[r]["rest"]
+            at = width_masked(r) + width_core(r)
+            nc.vector.tensor_scalar(
+                out=st[r]["w"][:, at : at + hi - lo], in0=logits[r][0][:, lo:hi], scalar1=-1.0,
+                scalar2=st[r]["tb"][:], op0=ALU.mult, op1=ALU.min, accum_out=t1[:],
+            )
+
+        def a_second(r):
+            lo = width_masked(r) + 512
+            nc.vector.tensor_scalar(
+                out=st[r]["w"][:, lo : lo + 512], in0=logits[r][1][:], scalar1=-1.0, scalar2=st[r]["t1"][:],
                 op0=ALU.mult, op1=ALU.min, accum_out=nm1s[:, r : r + 1],
             )
 
-        def bmask(r, n):
-            c0, c1 = window(r)
-            mo = c0 - (P * r - 256)
-            h, lo, hi = pieces_of(r)[n]
+        def mask_edges(r):
+            runs = []
+            for s, ms, key, w in lays[r]["edges"]:
+                if runs and runs[-1][0] + runs[-1][2] == s and runs[-1][1] + runs[-1][2] == ms:
+                    runs[-1][2] += w
+                else:
+                    runs.append([s, ms, w])
+            at = 0
+            for s, ms, w in runs:
+                nc.vector.tensor_tensor(
+                    out=st[r]["w"][:, at : at + w], in0=mask[:, ms : ms + w], in1=logits[r][0][:, s : s + w],
+                    op=ALU.subtract,
+                )
+                at += w
+
+        def mask_diag(r):
+            m = width_masked(r)
             nc.vector.tensor_tensor(
-                out=st[r]["ml"][:, lo - c0 : hi - c0],
-                in0=logits[r][h][:, lo - 512 * h : hi - 512 * h],
-                in1=mask[:, lo - c0 + mo : hi - c0 + mo],
-                op=ALU.add,
+                out=st[r]["w"][:, m - P : m], in0=mask[:, 2 * EDGE :], in1=logits[r][1][:, 0:P], op=ALU.subtract
             )
 
-        def cmax(r):
-            c0, c1 = window(r)
+        def min_masked(r):
+            m = width_masked(r)
             nm2 = small.tile([P, 1], F32, tag="nm2", name="nm2")
-            nc.vector.tensor_reduce(out=nm2[:], in_=st[r]["ml"][:, 0 : c1 - c0], axis=AX.X, op=ALU.max, negate=True)
+            scrap = work.tile([P, 400], F32, tag="scrap", name="scrap")
+            nc.vector.tensor_scalar(
+                out=scrap[:, 0:m], in0=st[r]["w"][:, 0:m], scalar1=1.0, scalar2=st[r]["tb"][:],
+                op0=ALU.mult, op1=ALU.min, accum_out=nm2[:],
+            )
             st[r]["nm2"] = nm2
+
+        def width_window(r):
+            return width_masked(r) + width_core(r)
+
+        def row_part(r):
+            m = width_masked(r)
+            return st[r]["w"][:, m : m + T]
 
         def exp1(r):
             e1 = work.tile([P, T], F32, tag="e1", name="e1")
             nc.scalar.activation(
-                out=e1[:], in_=st[r]["nl"][:], func=ACT.Exp, bias=nm1s[:, r : r + 1], scale=-1.0,
+                out=e1[:], in_=row_part(r), func=ACT.Exp, bias=nm1s[:, r : r + 1], scale=-1.0,
                 accum_out=z1[:, r : r + 1],
             )
             st[r]["e1"] = e1
 
         def exp2(r):
-            c0, c1 = window(r)
-            w = c1 - c0
+            w = width_window(r)
             e2 = work.tile([P, WIN], F32, tag="e2", name="e2")
             z2 = small.tile([P, 1], F32, tag="z2", name="z2")
             nc.scalar.activation(
-                out=e2[:, 0:w], in_=st[r]["ml"][:, 0:w], func=ACT.Exp, bias=st[r]["nm2"][:], scale=1.0, accum_out=z2[:]
+                out=e2[:, 0:w], in_=st[r]["w"][:, 0:w], func=ACT.Exp, bias=st[r]["nm2"][:], scale=-1.0, accum_out=z2[:]
             )
             st[r]["e2"] = e2
             st[r]["z2"] = z2
@@ -261,30 +379,45 @@ def tile_selfattention_pa_kernel(tc, q_bytes, q_scale, k, out_0, out_1, out_2):
             st[r]["rz2"] = rz2
 
         def norm(r, on_vector):
-            c0, c1 = window(r)
-            w = c1 - c0
+            w = width_window(r)
             att = work.tile([P, WIN], F32, tag="att", name="att")
             if on_vector:
                 nc.vector.tensor_scalar(
                     out=att[:, 0:w], in0=st[r]["e2"][:, 0:w], scalar1=st[r]["rz2"][:], scalar2=None, op0=ALU.mult
                 )
-            elif w == WIN:
-                nc.scalar.activation(out=att[:, 0:w], in_=st[r]["e2"][:, 0:w], func=ACT.Copy, scale=st[r]["rz2"][:])
             else:
-                nc.gpsimd.tensor_scalar(
-                    out=att[:, 0:w], in0=st[r]["e2"][:, 0:w], scalar1=st[r]["rz2"][:], scalar2=0.0,
-                    op0=ALU.mult, op1=ALU.add,
-                )
-            nc.sync.dma_start(out=out_0[P * r : P * (r + 1), c0:c1], in_=att[:, 0:w])
+                nc.scalar.activation(out=att[:, 0:w], in_=st[r]["e2"][:, 0:w], func=ACT.Copy, scale=st[r]["rz2"][:])
             st[r]["att"] = att
+            store_att(r)
+
+        def store_att(r):
+            att = st[r]["att"]
+            rows = slice(P * r, P * (r + 1))
+            at = 0
+            for s, ms, key, w in lays[r]["edges"]:
+                nc.sync.dma_start(out=out_0[rows, key : key + w], in_=att[:, at : at + w])
+                at += w
+            nc.sync.dma_start(out=out_0[rows, P * r : P * (r + 1)], in_=att[:, at : at + P])
+            at += P
+            core = lays[r]["core"]
+            if len(core) == 2:
+                step = core[1][1] - core[0][1]
+                v = max(0, min(core[0][1], T - 2 * step))
+                k0 = core[0][1] - v
+                nc.sync.dma_start(
+                    out=out_0[rows, v : v + 2 * step].rearrange("r (a c) -> r a c", c=step)[:, :, k0 : k0 + CORE],
+                    in_=att[:, at : at + 2 * CORE].rearrange("p (a c) -> p a c", a=2),
+                )
+            else:
+                nc.sync.dma_start(out=out_0[rows, core[0][1] : core[0][1] + CORE], in_=att[:, at : at + CORE])
 
         def prod_el(r):
             pr = work.tile([P, T], F32, tag="pr", name="pr")
-            nc.gpsimd.tensor_tensor(out=pr[:], in0=st[r]["e1"][:], in1=st[r]["nl"][:], op=ALU.mult)
+            nc.gpsimd.tensor_tensor(out=pr[:], in0=st[r]["e1"][:], in1=row_part(r), op=ALU.mult)
             st[r]["pr"] = pr
 
         def fold(r):
-            acc = psum.tile([P, 512], F32, tag="bank", name="fold")
+            acc = one_bank("fold")
             for b in range(NB):
                 nc.tensor.matmul(
                     acc[:, 0:P], lhsT=ident[:], rhs=st[r]["pr"][:, P * b : P * (b + 1)], start=(b == 0), stop=(b == NB - 1)
@@ -302,13 +435,12 @@ def tile_selfattention_pa_kernel(tc, q_bytes, q_scale, k, out_0, out_1, out_2):
         def prod_sum_vector(r):
             pr = work.tile([P, T], F32, tag="pr", name="pr")
             nc.vector.scalar_tensor_tensor(
-                out=pr[:], in0=st[r]["nl"][:], scalar=1.0, in1=st[r]["e1"][:], op0=ALU.mult, op1=ALU.mult,
+                out=pr[:], in0=row_part(r), scalar=1.0, in1=st[r]["e1"][:], op0=ALU.mult, op1=ALU.mult,
                 accum_out=s1[:, r : r + 1],
             )
 
         def pdiv(r):
-            c0, c1 = window(r)
-            w = c1 - c0
+            w = width_window(r)
             junk2 = work.tile([P, WIN], F32, tag="junk2", name="junk2")
             nc.vector.tensor_scalar(
                 out=junk2[:, 0:w], in0=st[r]["att"][:, 0:w], scalar1=1.0, scalar2=None,
@@ -327,14 +459,14 @@ def tile_selfattention_pa_kernel(tc, q_bytes, q_scale, k, out_0, out_1, out_2):
             nc.vector.tensor_tensor(out=mean[:], in0=s1[:], in1=rz1[:], op=ALU.mult)
             dsum = small.tile([P, 1], F32, tag="dsum", name="dsum")
             nc.vector.tensor_reduce(out=dsum[:], in_=fin[:, 0:NB], axis=AX.X, op=ALU.add, apply_absolute_value=True)
-            tot = psum.tile([P, 512], F32, tag="bank", name="tot")
+            tot = one_bank("tot")
             nc.tensor.matmul(tot[:, 0:1], lhsT=ones[:], rhs=dsum[:], start=True, stop=True)
             shifted = small.tile([P, NB], F32, tag="shifted", name="shifted")
             nc.vector.tensor_tensor(out=shifted[:], in0=mean[:], in1=nm1s[:], op=ALU.subtract)
             nc.vector.tensor_tensor(out=fin[:, 32 : 32 + NB], in0=lnz[:], in1=shifted[:], op=ALU.add)
             rtot = small.tile([P, 1], F32, tag="rtot", name="rtot")
             nc.vector.reciprocal(out=rtot[:], in_=tot[:, 0:1])
-            turned = psum.tile([P, 512], F32, tag="bank", name="turned")
+            turned = one_bank("turned")
             nc.tensor.transpose(turned[:, 0:P], fin[:], ident[:])
             res = const.tile([P, P], F32, name="res")
             nc.vector.tensor_scalar(
@@ -347,44 +479,65 @@ def tile_selfattention_pa_kernel(tc, q_bytes, q_scale, k, out_0, out_1, out_2):
             nc.sync.dma_start(out=out_2.rearrange("(r p) -> r p", p=P), in_=res[0:NB, :])
             nc.sync.dma_start(out=out_1.rearrange("(r p) -> r p", p=P), in_=res[32 : 32 + NB, :])
 
-        with tc.manual_schedule(engines={mybir.EngineType.DVE}):
-            widen_first()
-            q_turn(0, first[0])
-            q_turn(1, first[1])
-            k_front(0)
-            k_front(1)
-            qm(2)
-            k_front(2)
-            k_front(3)
-            qm(3)
-            qq(0)
-            qm(4)
-            k_front(4)
-            k_front(5)
-            qm(5)
-            qq(1)
-            k_quant(0)
-            k_front(6)
-            k_front(7)
-            qm(6)
-            k_quant(1)
-            qq(2)
-            mm(0)
-            qm(7)
-            mm(1)
         last = NB - 1
         with tc.manual_schedule():
+            cast(0, nc.vector)
+            cast(1, nc.vector)
+            cast(2, nc.scalar)
+            turn(0)
+            scale_out(0)
+            turn(1)
+            scale_out(1)
+            cast(3, nc.gpsimd)
+            turn(2)
+            scale_out(2)
+            turn(3)
+            scale_out(3)
+            k_turn(0)
+            k_copy(0)
+            k_turn(1)
+            k_copy(1)
+            k_turn(2)
+            k_copy(2)
+            k_turn(3)
+            k_copy(3)
+            cast(4, nc.gpsimd)
+            turn(4)
+            qq(0)
+            qq(1)
+            k_quant(0, 4)
+            scale_out(4)
+            cast(5, nc.gpsimd)
+            k_turn(4)
+            k_copy(4)
+            k_turn(5)
+            k_copy(5)
+            turn(5)
+            copy_out(5)
+            k_quant(4, 2)
+            k_turn(6)
+            k_copy(6)
+            k_turn(7)
+            k_copy(7)
+            cast(6, nc.gpsimd)
+            cast(7, nc.gpsimd)
+            scale_pool(5)
+            k_quant(6, 2)
+            turn(6)
+            copy_out(6)
+            mm(0)
+            scale_pool(6)
+            mm(1)
             for i in range(NB + 3):
                 if 2 <= i + 1 < NB:
                     mm(i + 1)
-                if 0 <= i - 3 < NFOLD:
+                if i == 1:
+                    turn(7)
+                if i - 3 in FOLDED:
                     fold(i - 3)
                 if 0 <= i - 1 < NB:
                     exp2(i - 1)
-                if i - 1 == last:
-                    log_z()
                 if 0 <= i - 2 < last:
-                    prod_el(i - 2)
                     norm(i - 2, False)
                 if i == 2:
                     zero_fill(0)
@@ -392,25 +545,39 @@ def tile_selfattention_pa_kernel(tc, q_bytes, q_scale, k, out_0, out_1, out_2):
                 if 2 <= i < NB:
                     zero_fill(i)
                 if i < NB:
-                    a1(i)
-                    for n in range(len(pieces_of(i))):
-                        bmask(i, n)
-                if 0 <= i - 3 < NFOLD:
-                    sum_fold(i - 3)
-                if NFOLD <= i - 2 < last:
-                    sum_el(i - 2)
+                    a_core(i, 0)
+                    mask_edges(i)
+                    a_core(i, 1)
+                    mask_diag(i)
+                    a_rest(i)
+                if i == 2:
+                    scale_pool(7)
+                if 0 <= i - 1 < ON_POOL:
+                    prod_el(i - 1)
+                if i - 4 in FOLDED:
+                    sum_fold(i - 4)
+                if 0 <= i - 3 < ON_POOL and i - 3 not in FOLDED:
+                    sum_el(i - 3)
                 if i < NB:
-                    a2(i)
+                    a_second(i)
                     exp1(i)
-                    cmax(i)
-                if i == 0:
-                    qq(3)
-                if 0 <= i - 3 < NB:
-                    pdiv(i - 3)
-                if i - 1 == last:
-                    prod_sum_vector(last)
-                if 0 <= i - 1 < NB:
+                    min_masked(i)
+                if i == 1:
+                    copy_out(7)
+                if 0 <= i - 1 < last:
                     rcp(i - 1)
+                if i == 1:
+                    qq(2)
+                if i == 3:
+                    qq(3)
                 if i - 1 == last:
+                    prod_sum_vector(last - 1)
+                    prod_sum_vector(last)
+                    rcp(last)
                     norm(last, True)
+                if 0 <= i - 2 < last:
+                    pdiv(i - 2)
+                if i - 2 == last:
+                    log_z()
+                    pdiv(last)
             finish()

@@ -25,6 +25,7 @@ WIN = 640
 EDGE = 136
 BIG = 2.0 ** 100
 FOLDED = (1, 2, 3, 4)
+SUMMED = {3: 0, 7: 5}
 ON_POOL = 6
 
 
@@ -103,6 +104,8 @@ def tile_selfattention_pa_kernel(tc, q_bytes, q_scale, k, out_0, out_1, out_2):
         nc.vector.memset(ones[:], 1.0)
         fin = const.tile([P, P], F32, name="fin")
         nc.vector.memset(fin[:], 0.0)
+        ent = const.tile([P, P], F32, name="ent")
+        nc.vector.memset(ent[:], 0.0)
 
         z1 = const.tile([P, NB], F32, name="z1")
         s1 = const.tile([P, NB], F32, name="s1")
@@ -385,8 +388,13 @@ def tile_selfattention_pa_kernel(tc, q_bytes, q_scale, k, out_0, out_1, out_2):
                 nc.vector.tensor_scalar(
                     out=att[:, 0:w], in0=st[r]["e2"][:, 0:w], scalar1=st[r]["rz2"][:], scalar2=None, op0=ALU.mult
                 )
-            else:
+            elif r < last - 1:
                 nc.scalar.activation(out=att[:, 0:w], in_=st[r]["e2"][:, 0:w], func=ACT.Copy, scale=st[r]["rz2"][:])
+            else:
+                nc.gpsimd.tensor_scalar(
+                    out=att[:, 0:w], in0=st[r]["e2"][:, 0:w], scalar1=st[r]["rz2"][:], scalar2=0.0,
+                    op0=ALU.mult, op1=ALU.add,
+                )
             st[r]["att"] = att
             store_att(r)
 
@@ -452,32 +460,36 @@ def tile_selfattention_pa_kernel(tc, q_bytes, q_scale, k, out_0, out_1, out_2):
         def log_z():
             nc.scalar.activation(out=lnz[:], in_=z1[:], func=ACT.Ln)
 
-        def finish():
+        shifted = const.tile([P, NB], F32, name="shifted")
+
+        def mean_el():
             rz1 = small.tile([P, NB], F32, tag="rz1", name="rz1")
             nc.vector.reciprocal(out=rz1[:], in_=z1[:])
             mean = small.tile([P, NB], F32, tag="mean", name="mean")
             nc.vector.tensor_tensor(out=mean[:], in0=s1[:], in1=rz1[:], op=ALU.mult)
-            dsum = small.tile([P, 1], F32, tag="dsum", name="dsum")
-            nc.vector.tensor_reduce(out=dsum[:], in_=fin[:, 0:NB], axis=AX.X, op=ALU.add, apply_absolute_value=True)
-            tot = one_bank("tot")
-            nc.tensor.matmul(tot[:, 0:1], lhsT=ones[:], rhs=dsum[:], start=True, stop=True)
-            shifted = small.tile([P, NB], F32, tag="shifted", name="shifted")
             nc.vector.tensor_tensor(out=shifted[:], in0=mean[:], in1=nm1s[:], op=ALU.subtract)
-            nc.vector.tensor_tensor(out=fin[:, 32 : 32 + NB], in0=lnz[:], in1=shifted[:], op=ALU.add)
-            rtot = small.tile([P, 1], F32, tag="rtot", name="rtot")
-            nc.vector.reciprocal(out=rtot[:], in_=tot[:, 0:1])
+
+        def finish():
+            tot = one_bank("tot")
+            for r in range(NB):
+                nc.tensor.matmul(tot[:, 0:1], lhsT=ones[:], rhs=fin[:, r : r + 1], start=(r == 0), stop=(r == last))
             turned = one_bank("turned")
             nc.tensor.transpose(turned[:, 0:P], fin[:], ident[:])
-            res = const.tile([P, P], F32, name="res")
+            nc.vector.tensor_tensor(out=ent[:, 0:NB], in0=lnz[:], in1=shifted[:], op=ALU.add)
+            rtot = small.tile([P, 1], F32, tag="rtot", name="rtot")
+            nc.vector.reciprocal(out=rtot[:], in_=tot[:, 0:1])
+            turned2 = one_bank("turned2")
+            nc.tensor.transpose(turned2[:, 0:P], ent[:], ident[:])
+            res = const.tile([NB, P], F32, name="res")
             nc.vector.tensor_scalar(
-                out=res[0:NB, :], in0=turned[0:NB, 0:P], scalar1=rtot[0:NB, :], scalar2=None, op0=ALU.mult
+                out=res[:], in0=turned[0:NB, 0:P], scalar1=rtot[0:NB, :], scalar2=None, op0=ALU.mult
             )
+            nc.sync.dma_start(out=out_2.rearrange("(r p) -> r p", p=P), in_=res[:])
+            res2 = const.tile([NB, P], F32, name="res2")
             nc.scalar.activation(
-                out=res[32 : 32 + NB, :], in_=turned[32 : 32 + NB, 0:P], func=ACT.Copy,
-                scale=1.0 / math.log(float(T)),
+                out=res2[:], in_=turned2[0:NB, 0:P], func=ACT.Copy, scale=1.0 / math.log(float(T)),
             )
-            nc.sync.dma_start(out=out_2.rearrange("(r p) -> r p", p=P), in_=res[0:NB, :])
-            nc.sync.dma_start(out=out_1.rearrange("(r p) -> r p", p=P), in_=res[32 : 32 + NB, :])
+            nc.scalar.dma_start(out=out_1.rearrange("(r p) -> r p", p=P), in_=res2[:])
 
         last = NB - 1
         with tc.manual_schedule():
@@ -548,20 +560,23 @@ def tile_selfattention_pa_kernel(tc, q_bytes, q_scale, k, out_0, out_1, out_2):
                     a_core(i, 0)
                     mask_edges(i)
                     a_core(i, 1)
-                    mask_diag(i)
+                if 0 <= i - 3 < last:
+                    pdiv(i - 3)
+                if i < NB:
                     a_rest(i)
+                    mask_diag(i)
                 if i == 2:
                     scale_pool(7)
                 if 0 <= i - 1 < ON_POOL:
                     prod_el(i - 1)
-                if i - 4 in FOLDED:
-                    sum_fold(i - 4)
-                if 0 <= i - 3 < ON_POOL and i - 3 not in FOLDED:
-                    sum_el(i - 3)
                 if i < NB:
                     a_second(i)
                     exp1(i)
                     min_masked(i)
+                if i - 4 in FOLDED:
+                    sum_fold(i - 4)
+                if i in SUMMED:
+                    sum_el(SUMMED[i])
                 if i == 1:
                     copy_out(7)
                 if 0 <= i - 1 < last:
@@ -575,9 +590,8 @@ def tile_selfattention_pa_kernel(tc, q_bytes, q_scale, k, out_0, out_1, out_2):
                     prod_sum_vector(last)
                     rcp(last)
                     norm(last, True)
-                if 0 <= i - 2 < last:
-                    pdiv(i - 2)
                 if i - 2 == last:
                     log_z()
+                    mean_el()
                     pdiv(last)
             finish()

@@ -489,7 +489,7 @@ def tile_selfattention_pa_kernel(tc, q_bytes, q_scale, k, out_0, out_1, out_2):
             nc.scalar.activation(
                 out=res2[:], in_=turned2[0:NB, 0:P], func=ACT.Copy, scale=1.0 / math.log(float(T)),
             )
-            nc.scalar.dma_start(out=out_1.rearrange("(r p) -> r p", p=P), in_=res2[:])
+            nc.sync.dma_start(out=out_1.rearrange("(r p) -> r p", p=P), in_=res2[:])
 
         last = NB - 1
         with tc.manual_schedule():

@@ -388,13 +388,8 @@ def tile_selfattention_pa_kernel(tc, q_bytes, q_scale, k, out_0, out_1, out_2):
                 nc.vector.tensor_scalar(
                     out=att[:, 0:w], in0=st[r]["e2"][:, 0:w], scalar1=st[r]["rz2"][:], scalar2=None, op0=ALU.mult
                 )
-            elif r < last - 1:
-                nc.scalar.activation(out=att[:, 0:w], in_=st[r]["e2"][:, 0:w], func=ACT.Copy, scale=st[r]["rz2"][:])
             else:
-                nc.gpsimd.tensor_scalar(
-                    out=att[:, 0:w], in0=st[r]["e2"][:, 0:w], scalar1=st[r]["rz2"][:], scalar2=0.0,
-                    op0=ALU.mult, op1=ALU.add,
-                )
+                nc.scalar.activation(out=att[:, 0:w], in_=st[r]["e2"][:, 0:w], func=ACT.Copy, scale=st[r]["rz2"][:])
             st[r]["att"] = att
             store_att(r)
 
@@ -500,13 +495,13 @@ def tile_selfattention_pa_kernel(tc, q_bytes, q_scale, k, out_0, out_1, out_2):
             scale_out(0)
             turn(1)
             scale_out(1)
-            cast(3, nc.gpsimd)
+            cast(3, nc.scalar)
             turn(2)
             scale_out(2)
-            turn(3)
-            scale_out(3)
             k_turn(0)
             k_copy(0)
+            turn(3)
+            scale_out(3)
             k_turn(1)
             k_copy(1)
             k_turn(2)
@@ -549,7 +544,7 @@ def tile_selfattention_pa_kernel(tc, q_bytes, q_scale, k, out_0, out_1, out_2):
                     fold(i - 3)
                 if 0 <= i - 1 < NB:
                     exp2(i - 1)
-                if 0 <= i - 2 < last:
+                if 0 <= i - 2 < last - 1:
                     norm(i - 2, False)
                 if i == 2:
                     zero_fill(0)
@@ -560,6 +555,8 @@ def tile_selfattention_pa_kernel(tc, q_bytes, q_scale, k, out_0, out_1, out_2):
                     a_core(i, 0)
                     mask_edges(i)
                     a_core(i, 1)
+                if i - 1 == last:
+                    norm(last - 1, True)
                 if 0 <= i - 3 < last:
                     pdiv(i - 3)
                 if i < NB:

@@ -68,9 +68,9 @@ def tile_selfattention_pa_kernel(tc, q_bytes, q_scale, k, out_0, out_1, out_2):
         load_q_pair(1)
         load_k(0)
         load_k(1)
+        load_q_pair(2)
         load_k(2)
         load_k(3)
-        load_q_pair(2)
         load_k(4)
         load_k(5)
         load_k(6)
@@ -134,10 +134,11 @@ def tile_selfattention_pa_kernel(tc, q_bytes, q_scale, k, out_0, out_1, out_2):
                         bank[:, P * (2 * g + u) : P * (2 * g + u + 1)], words[:, 256 * g + u : 256 * (g + 1) : 2], ident[:]
                     )
 
-        gq = []
-        for i in range(NB // 2):
-            g_pair = const.tile([P, 2 * D], BF16, name="gq%d" % i, align_bytes=64)
-            gq.append(g_pair)
+        gq = {}
+
+        def new_pair(i):
+            gq[i] = stage.tile([P, 2 * D], BF16, tag="late" if i >= 2 else "early", name="gq", align_bytes=64, bufs=1 if i >= 2 else 2)
+
         qbf = {}
         qbank = {}
         kbank = {}
@@ -158,6 +159,8 @@ def tile_selfattention_pa_kernel(tc, q_bytes, q_scale, k, out_0, out_1, out_2):
             qbank[b] = bank
 
         def scale_out(b):
+            if b % 2 == 0:
+                new_pair(b // 2)
             for g in range(2):
                 lo = D * (b % 2) + 512 * g
                 nc.vector.tensor_tensor(
@@ -176,6 +179,8 @@ def tile_selfattention_pa_kernel(tc, q_bytes, q_scale, k, out_0, out_1, out_2):
             graw[b] = t
 
         def scale_pool(b):
+            if b % 2 == 0:
+                new_pair(b // 2)
             lo = D * (b % 2)
             nc.gpsimd.tensor_tensor(
                 out=gq[b // 2][:, lo : lo + D].rearrange("p (g r t) -> p g r t", g=2, t=4),
@@ -415,7 +420,10 @@ def tile_selfattention_pa_kernel(tc, q_bytes, q_scale, k, out_0, out_1, out_2):
                 nc.sync.dma_start(out=out_0[rows, core[0][1] : core[0][1] + CORE], in_=att[:, at : at + CORE])
 
         def prod_el(r):
-            pr = work.tile([P, T], F32, tag="pr", name="pr")
+            if r == 0:
+                pr = stage.tile([P, T], F32, tag="late", name="pr", align_bytes=64, bufs=1)
+            else:
+                pr = work.tile([P, T], F32, tag="pr", name="pr")
             nc.gpsimd.tensor_tensor(out=pr[:], in0=st[r]["e1"][:], in1=row_part(r), op=ALU.mult)
             st[r]["pr"] = pr
 
@@ -502,44 +510,45 @@ def tile_selfattention_pa_kernel(tc, q_bytes, q_scale, k, out_0, out_1, out_2):
             k_copy(0)
             turn(3)
             scale_out(3)
+            cast(4, nc.gpsimd)
             k_turn(1)
             k_copy(1)
             k_turn(2)
             k_copy(2)
-            k_turn(3)
-            k_copy(3)
-            cast(4, nc.gpsimd)
             turn(4)
-            qq(0)
-            qq(1)
-            k_quant(0, 4)
             scale_out(4)
             cast(5, nc.gpsimd)
+            k_turn(3)
+            k_copy(3)
+            turn(5)
+            scale_out(5)
+            cast(6, nc.gpsimd)
             k_turn(4)
             k_copy(4)
             k_turn(5)
             k_copy(5)
-            turn(5)
-            copy_out(5)
-            k_quant(4, 2)
             k_turn(6)
             k_copy(6)
             k_turn(7)
             k_copy(7)
-            cast(6, nc.gpsimd)
-            cast(7, nc.gpsimd)
-            scale_pool(5)
+            cast(7, nc.scalar)
+            qq(0)
+            k_quant(0, 4)
+            k_quant(4, 2)
             k_quant(6, 2)
+            qq(1)
+            qq(2)
             turn(6)
             copy_out(6)
             mm(0)
             scale_pool(6)
+            turn(7)
+            copy_out(7)
+            scale_pool(7)
             mm(1)
             for i in range(NB + 3):
-                if 2 <= i + 1 < NB:
-                    mm(i + 1)
-                if i == 1:
-                    turn(7)
+                if i + 2 < NB:
+                    mm(i + 2)
                 if i - 3 in FOLDED:
                     fold(i - 3)
                 if 0 <= i - 1 < NB:
@@ -562,26 +571,21 @@ def tile_selfattention_pa_kernel(tc, q_bytes, q_scale, k, out_0, out_1, out_2):
                 if i < NB:
                     a_rest(i)
                     mask_diag(i)
-                if i == 2:
-                    scale_pool(7)
-                if 0 <= i - 1 < ON_POOL:
-                    prod_el(i - 1)
                 if i < NB:
                     a_second(i)
                     exp1(i)
                     min_masked(i)
+                if i == 2:
+                    qq(3)
+                    prod_el(0)
+                if 1 <= i - 1 < ON_POOL:
+                    prod_el(i - 1)
                 if i - 4 in FOLDED:
                     sum_fold(i - 4)
                 if i in SUMMED:
                     sum_el(SUMMED[i])
-                if i == 1:
-                    copy_out(7)
                 if 0 <= i - 1 < last:
                     rcp(i - 1)
-                if i == 1:
-                    qq(2)
-                if i == 3:
-                    qq(3)
                 if i - 1 == last:
                     prod_sum_vector(last - 1)
                     prod_sum_vector(last)

@@ -36,10 +36,14 @@ def tile_selfattention_pa_kernel(tc, q_bytes, q_scale, k, out_0, out_1, out_2):
         stage = ctx.enter_context(tc.tile_pool(name="stage", bufs=4))
         work = ctx.enter_context(tc.tile_pool(name="work", bufs=4))
         small = ctx.enter_context(tc.tile_pool(name="small", bufs=4))
-        psum = ctx.enter_context(tc.psum_pool(name="psum", bufs=8))
+        psum = ctx.enter_context(tc.psum_pool(name="psum", bufs=2))
+        psum2 = ctx.enter_context(tc.psum_pool(name="psum2", bufs=3))
 
         def one_bank(name):
             return psum.tile([P, 512], F32, tag="bank", name=name)
+
+        def two_banks(name):
+            return psum2.tile([P, 2, 512], F32, tag="banks", name=name)
 
         sct = const.tile([P, 2, 4], F32, name="sct")
         qbytes = []
@@ -154,7 +158,7 @@ def tile_selfattention_pa_kernel(tc, q_bytes, q_scale, k, out_0, out_1, out_2):
             qbf[b] = t
 
         def turn(b):
-            bank = one_bank("turn")
+            bank = two_banks("turn")[:, 0, :] if b == 2 else one_bank("turn")[:]
             transposes(qbf[b][:], bank)
             qbank[b] = bank
 
@@ -174,7 +178,7 @@ def tile_selfattention_pa_kernel(tc, q_bytes, q_scale, k, out_0, out_1, out_2):
             t = stage.tile([P, D], BF16, tag="graw", name="graw")
             nc.scalar.copy(
                 out=t[:].bitcast(F32).rearrange("p (g r u) -> p g r u", g=2, u=2),
-                in_=qbank[b][:].rearrange("p (g u r) -> p g r u", g=2, u=2),
+                in_=qbank[b].rearrange("p (g u r) -> p g r u", g=2, u=2),
             )
             graw[b] = t
 
@@ -193,7 +197,7 @@ def tile_selfattention_pa_kernel(tc, q_bytes, q_scale, k, out_0, out_1, out_2):
             nc.vector.quantize_mx(out=qc[pair][:].bitcast(FP8X4), scales=qs[pair][:], in_=gq[pair][:])
 
         def k_turn(b):
-            kbank[b] = one_bank("kturn")
+            kbank[b] = two_banks("kturn")[:, 0, :] if True else one_bank("kturn")[:]
             transposes(kraw[b][:], kbank[b])
 
         def k_copy(b):
@@ -202,7 +206,7 @@ def tile_selfattention_pa_kernel(tc, q_bytes, q_scale, k, out_0, out_1, out_2):
             j = b - b0
             gw = gk[b0][:].rearrange("p g c -> p (g c)").bitcast(F32).rearrange("p (g r u) -> p g r u", g=2, u=2)
             nc.scalar.copy(
-                out=gw[:, :, P * j : P * (j + 1), :], in_=bank[:].rearrange("p (g u r) -> p g r u", g=2, u=2)
+                out=gw[:, :, P * j : P * (j + 1), :], in_=bank.rearrange("p (g u r) -> p g r u", g=2, u=2)
             )
 
         def k_quant(b, n):
@@ -244,10 +248,10 @@ def tile_selfattention_pa_kernel(tc, q_bytes, q_scale, k, out_0, out_1, out_2):
                     edges.append((384, EDGE + P, 0, EDGE - P))
             lay["edges"] = edges
             core = []
-            if r > 0:
-                core.append((512 - CORE, base + EDGE))
             if r + 1 < NB:
                 core.append((0, P * (r + 1)))
+            if r > 0:
+                core.append((512 - CORE, base + EDGE))
             lay["core"] = core
             lay["rest"] = (CORE if r + 1 < NB else 0, 512 - CORE if r > 0 else 512)
             return lay
@@ -270,13 +274,13 @@ def tile_selfattention_pa_kernel(tc, q_bytes, q_scale, k, out_0, out_1, out_2):
             return out
 
         def mm(r):
-            logits[r] = []
+            acc = two_banks("acc")
+            logits[r] = acc
             for h in range(2):
-                acc = one_bank("acc")
                 for place, blk, n in runs_of(lays[r]["banks"][h]):
                     for g in range(2):
                         nc.tensor.matmul_mx(
-                            out=acc[:, P * place : P * (place + n)],
+                            out=acc[:, h, P * place : P * (place + n)],
                             lhsT=qc[r // 2][:, 256 * (r % 2) + P * g : 256 * (r % 2) + P * (g + 1)].bitcast(FP8X4),
                             lhsT_scale=qs[r // 2][:, 256 * (r % 2) + P * g : 256 * (r % 2) + P * (g + 1)],
                             rhs=kc[:, g, P * blk : P * (blk + n)].bitcast(FP8X4),
@@ -284,7 +288,6 @@ def tile_selfattention_pa_kernel(tc, q_bytes, q_scale, k, out_0, out_1, out_2):
                             start=(g == 0),
                             stop=(g == 1),
                         )
-                logits[r].append(acc)
 
         def width_masked(r):
             return P + sum(e[3] for e in lays[r]["edges"])
@@ -292,21 +295,23 @@ def tile_selfattention_pa_kernel(tc, q_bytes, q_scale, k, out_0, out_1, out_2):
         def width_core(r):
             return CORE * len(lays[r]["core"])
 
-        def a_core(r, c):
-            if c == 0:
-                work_w = work.tile([P, 400 + T], F32, tag="w", name="w")
-                st[r] = {"w": work_w, "tb": None}
-            if c >= len(lays[r]["core"]):
-                return
+        def a_core(r):
+            work_w = work.tile([P, 1 + 400 + T], F32, tag="w", name="w")
+            st[r] = {"lead": work_w, "w": work_w[:, 1:]}
             m = width_masked(r)
-            tb = st[r]["tb"]
-            t_new = small.tile([P, 1], F32, tag="tb%d" % c, name="tb")
-            s = lays[r]["core"][c][0]
+            core = lays[r]["core"]
+            out = st[r]["w"][:, m : m + CORE * len(core)]
+            if len(core) == 2:
+                step = 512 - CORE
+                flat = logits[r][:].rearrange("p b c -> p (b c)")
+                src = flat[:, 0 : 2 * step].rearrange("p (a c) -> p a c", c=step)[:, :, 0:CORE]
+                out = out.rearrange("p (a c) -> p a c", a=2)
+            else:
+                src = logits[r][:, 0, core[0][0] : core[0][0] + CORE]
             nc.vector.tensor_scalar(
-                out=st[r]["w"][:, m + CORE * c : m + CORE * (c + 1)], in0=logits[r][0][:, s : s + CORE], scalar1=-1.0,
-                scalar2=None if tb is None else tb[:], op0=ALU.mult, op1=ALU.min, accum_out=t_new[:],
+                out=out, in0=src, scalar1=-1.0, scalar2=None, op0=ALU.mult, op1=ALU.min,
+                accum_out=work_w[:, 0:1],
             )
-            st[r]["tb"] = t_new
 
         def a_rest(r):
             t1 = small.tile([P, 1], F32, tag="t1", name="t1")
@@ -314,14 +319,14 @@ def tile_selfattention_pa_kernel(tc, q_bytes, q_scale, k, out_0, out_1, out_2):
             lo, hi = lays[r]["rest"]
             at = width_masked(r) + width_core(r)
             nc.vector.tensor_scalar(
-                out=st[r]["w"][:, at : at + hi - lo], in0=logits[r][0][:, lo:hi], scalar1=-1.0,
-                scalar2=st[r]["tb"][:], op0=ALU.mult, op1=ALU.min, accum_out=t1[:],
+                out=st[r]["w"][:, at : at + hi - lo], in0=logits[r][:, 0, lo:hi], scalar1=-1.0,
+                scalar2=st[r]["lead"][:, 0:1], op0=ALU.mult, op1=ALU.min, accum_out=t1[:],
             )
 
         def a_second(r):
             lo = width_masked(r) + 512
             nc.vector.tensor_scalar(
-                out=st[r]["w"][:, lo : lo + 512], in0=logits[r][1][:], scalar1=-1.0, scalar2=st[r]["t1"][:],
+                out=st[r]["w"][:, lo : lo + 512], in0=logits[r][:, 1, :], scalar1=-1.0, scalar2=st[r]["t1"][:],
                 op0=ALU.mult, op1=ALU.min, accum_out=nm1s[:, r : r + 1],
             )
 
@@ -335,7 +340,7 @@ def tile_selfattention_pa_kernel(tc, q_bytes, q_scale, k, out_0, out_1, out_2):
             at = 0
             for s, ms, w in runs:
                 nc.vector.tensor_tensor(
-                    out=st[r]["w"][:, at : at + w], in0=mask[:, ms : ms + w], in1=logits[r][0][:, s : s + w],
+                    out=st[r]["w"][:, at : at + w], in0=mask[:, ms : ms + w], in1=logits[r][:, 0, s : s + w],
                     op=ALU.subtract,
                 )
                 at += w
@@ -343,17 +348,13 @@ def tile_selfattention_pa_kernel(tc, q_bytes, q_scale, k, out_0, out_1, out_2):
         def mask_diag(r):
             m = width_masked(r)
             nc.vector.tensor_tensor(
-                out=st[r]["w"][:, m - P : m], in0=mask[:, 2 * EDGE :], in1=logits[r][1][:, 0:P], op=ALU.subtract
+                out=st[r]["w"][:, m - P : m], in0=mask[:, 2 * EDGE :], in1=logits[r][:, 1, 0:P], op=ALU.subtract
             )
 
         def min_masked(r):
             m = width_masked(r)
             nm2 = small.tile([P, 1], F32, tag="nm2", name="nm2")
-            scrap = work.tile([P, 400], F32, tag="scrap", name="scrap")
-            nc.vector.tensor_scalar(
-                out=scrap[:, 0:m], in0=st[r]["w"][:, 0:m], scalar1=1.0, scalar2=st[r]["tb"][:],
-                op0=ALU.mult, op1=ALU.min, accum_out=nm2[:],
-            )
+            nc.vector.tensor_reduce(out=nm2[:], in_=st[r]["lead"][:, 0 : 1 + m], axis=AX.X, op=ALU.min)
             st[r]["nm2"] = nm2
 
         def width_window(r):
@@ -407,17 +408,9 @@ def tile_selfattention_pa_kernel(tc, q_bytes, q_scale, k, out_0, out_1, out_2):
                 at += w
             nc.sync.dma_start(out=out_0[rows, P * r : P * (r + 1)], in_=att[:, at : at + P])
             at += P
-            core = lays[r]["core"]
-            if len(core) == 2:
-                step = core[1][1] - core[0][1]
-                v = max(0, min(core[0][1], T - 2 * step))
-                k0 = core[0][1] - v
-                nc.sync.dma_start(
-                    out=out_0[rows, v : v + 2 * step].rearrange("r (a c) -> r a c", c=step)[:, :, k0 : k0 + CORE],
-                    in_=att[:, at : at + 2 * CORE].rearrange("p (a c) -> p a c", a=2),
-                )
-            else:
-                nc.sync.dma_start(out=out_0[rows, core[0][1] : core[0][1] + CORE], in_=att[:, at : at + CORE])
+            for start, key in lays[r]["core"]:
+                nc.sync.dma_start(out=out_0[rows, key : key + CORE], in_=att[:, at : at + CORE])
+                at += CORE
 
         def prod_el(r):
             if r == 0:
@@ -476,7 +469,7 @@ def tile_selfattention_pa_kernel(tc, q_bytes, q_scale, k, out_0, out_1, out_2):
             tot = one_bank("tot")
             for r in range(NB):
                 nc.tensor.matmul(tot[:, 0:1], lhsT=ones[:], rhs=fin[:, r : r + 1], start=(r == 0), stop=(r == last))
-            turned = one_bank("turned")
+            turned = two_banks("turned")[:, 0, :]
             nc.tensor.transpose(turned[:, 0:P], fin[:], ident[:])
             nc.vector.tensor_tensor(out=ent[:, 0:NB], in0=lnz[:], in1=shifted[:], op=ALU.add)
             rtot = small.tile([P, 1], F32, tag="rtot", name="rtot")
@@ -513,10 +506,10 @@ def tile_selfattention_pa_kernel(tc, q_bytes, q_scale, k, out_0, out_1, out_2):
             cast(4, nc.gpsimd)
             k_turn(1)
             k_copy(1)
-            k_turn(2)
-            k_copy(2)
             turn(4)
             scale_out(4)
+            k_turn(2)
+            k_copy(2)
             cast(5, nc.gpsimd)
             k_turn(3)
             k_copy(3)
@@ -561,9 +554,8 @@ def tile_selfattention_pa_kernel(tc, q_bytes, q_scale, k, out_0, out_1, out_2):
                 if 2 <= i < NB:
                     zero_fill(i)
                 if i < NB:
-                    a_core(i, 0)
+                    a_core(i)
                     mask_edges(i)
-                    a_core(i, 1)
                 if i - 1 == last:
                     norm(last - 1, True)
                 if 0 <= i - 3 < last:

@@ -25,7 +25,7 @@ WIN = 640
 EDGE = 136
 BIG = 2.0 ** 100
 FOLDED = (1, 2, 3, 4)
-SUMMED = {3: 0, 7: 5}
+SUMMED = {4: 0}
 ON_POOL = 6
 
 
@@ -75,11 +75,11 @@ def tile_selfattention_pa_kernel(tc, q_bytes, q_scale, k, out_0, out_1, out_2):
         load_q_pair(2)
         load_k(2)
         load_k(3)
+        load_q_pair(3)
         load_k(4)
         load_k(5)
         load_k(6)
         load_k(7)
-        load_q_pair(3)
 
         warm = const.tile([P, 1], F32, name="warm")
         warm2 = const.tile([P, 1], F32, name="warm2")
@@ -457,33 +457,47 @@ def tile_selfattention_pa_kernel(tc, q_bytes, q_scale, k, out_0, out_1, out_2):
             nc.scalar.activation(out=lnz[:], in_=z1[:], func=ACT.Ln)
 
         shifted = const.tile([P, NB], F32, name="shifted")
+        rz1 = const.tile([P, NB], F32, name="rz1")
+        mean = const.tile([P, NB], F32, name="mean")
 
-        def mean_el():
-            rz1 = small.tile([P, NB], F32, tag="rz1", name="rz1")
+        def row_log():
+            nc.vector.tensor_tensor(out=shifted[:], in0=lnz[:], in1=nm1s[:], op=ALU.subtract)
+
+        def row_inverse():
             nc.vector.reciprocal(out=rz1[:], in_=z1[:])
-            mean = small.tile([P, NB], F32, tag="mean", name="mean")
-            nc.vector.tensor_tensor(out=mean[:], in0=s1[:], in1=rz1[:], op=ALU.mult)
-            nc.vector.tensor_tensor(out=shifted[:], in0=mean[:], in1=nm1s[:], op=ALU.subtract)
 
-        def finish():
+        def row_mean():
+            nc.vector.tensor_tensor(out=mean[:], in0=s1[:], in1=rz1[:], op=ALU.mult)
+
+        rtot = const.tile([P, 1], F32, name="rtot")
+        turned = {}
+
+        def div_out():
             tot = one_bank("tot")
             for r in range(NB):
                 nc.tensor.matmul(tot[:, 0:1], lhsT=ones[:], rhs=fin[:, r : r + 1], start=(r == 0), stop=(r == last))
-            turned = two_banks("turned")[:, 0, :]
-            nc.tensor.transpose(turned[:, 0:P], fin[:], ident[:])
-            nc.vector.tensor_tensor(out=ent[:, 0:NB], in0=lnz[:], in1=shifted[:], op=ALU.add)
-            rtot = small.tile([P, 1], F32, tag="rtot", name="rtot")
-            nc.vector.reciprocal(out=rtot[:], in_=tot[:, 0:1])
-            turned2 = one_bank("turned2")
-            nc.tensor.transpose(turned2[:, 0:P], ent[:], ident[:])
+            turned[0] = two_banks("turned")[:, 0, :]
+            nc.tensor.transpose(turned[0][:, 0:P], fin[:], ident[:])
+            turned["tot"] = tot
+
+        def div_store():
+            nc.vector.reciprocal(out=rtot[:], in_=turned["tot"][:, 0:1])
             res = const.tile([NB, P], F32, name="res")
             nc.vector.tensor_scalar(
-                out=res[:], in0=turned[0:NB, 0:P], scalar1=rtot[0:NB, :], scalar2=None, op0=ALU.mult
+                out=res[:], in0=turned[0][0:NB, 0:P], scalar1=rtot[0:NB, :], scalar2=None, op0=ALU.mult
             )
             nc.sync.dma_start(out=out_2.rearrange("(r p) -> r p", p=P), in_=res[:])
+
+        def entropy_out():
+            nc.vector.tensor_tensor(out=ent[:, 0:NB], in0=mean[:], in1=shifted[:], op=ALU.add)
+            turned2 = one_bank("turned2")
+            nc.tensor.transpose(turned2[:, 0:P], ent[:], ident[:])
+            turned[1] = turned2
+
+        def entropy_store():
             res2 = const.tile([NB, P], F32, name="res2")
             nc.scalar.activation(
-                out=res2[:], in_=turned2[0:NB, 0:P], func=ACT.Copy, scale=1.0 / math.log(float(T)),
+                out=res2[:], in_=turned[1][0:NB, 0:P], func=ACT.Copy, scale=1.0 / math.log(float(T)),
             )
             nc.sync.dma_start(out=out_1.rearrange("(r p) -> r p", p=P), in_=res2[:])
 
@@ -539,34 +553,33 @@ def tile_selfattention_pa_kernel(tc, q_bytes, q_scale, k, out_0, out_1, out_2):
             copy_out(7)
             scale_pool(7)
             mm(1)
-            for i in range(NB + 3):
+            for i in range(NB):
                 if i + 2 < NB:
                     mm(i + 2)
                 if i - 3 in FOLDED:
                     fold(i - 3)
-                if 0 <= i - 1 < NB:
+                if i >= 1:
                     exp2(i - 1)
-                if 0 <= i - 2 < last - 1:
+                if i >= 2:
                     norm(i - 2, False)
                 if i == 2:
                     zero_fill(0)
                     zero_fill(1)
-                if 2 <= i < NB:
+                if i >= 2:
                     zero_fill(i)
-                if i < NB:
-                    a_core(i)
-                    mask_edges(i)
-                if i - 1 == last:
-                    norm(last - 1, True)
-                if 0 <= i - 3 < last:
+                a_core(i)
+                mask_edges(i)
+                if i >= 3:
                     pdiv(i - 3)
-                if i < NB:
-                    a_rest(i)
-                    mask_diag(i)
-                if i < NB:
-                    a_second(i)
+                a_rest(i)
+                mask_diag(i)
+                a_second(i)
+                if i < last:
                     exp1(i)
-                    min_masked(i)
+                min_masked(i)
+                if i == last:
+                    exp2(i)
+                    exp1(i)
                 if i == 2:
                     qq(3)
                     prod_el(0)
@@ -576,15 +589,23 @@ def tile_selfattention_pa_kernel(tc, q_bytes, q_scale, k, out_0, out_1, out_2):
                     sum_fold(i - 4)
                 if i in SUMMED:
                     sum_el(SUMMED[i])
-                if 0 <= i - 1 < last:
+                if i >= 1:
                     rcp(i - 1)
-                if i - 1 == last:
-                    prod_sum_vector(last - 1)
-                    prod_sum_vector(last)
-                    rcp(last)
-                    norm(last, True)
-                if i - 2 == last:
-                    log_z()
-                    mean_el()
-                    pdiv(last)
-            finish()
+            pdiv(last - 2)
+            norm(last - 1, True)
+            rcp(last)
+            log_z()
+            sum_el(last - 2)
+            sum_fold(last - 3)
+            pdiv(last - 1)
+            norm(last, True)
+            prod_sum_vector(last - 1)
+            row_inverse()
+            prod_sum_vector(last)
+            row_log()
+            pdiv(last)
+            row_mean()
+            div_out()
+            entropy_out()
+            div_store()
+            entropy_store()

@@ -24,7 +24,7 @@ BAND = 250
 WIN = 640
 EDGE = 136
 BIG = 2.0 ** 100
-FOLDED = (1, 2, 3, 4)
+FOLDED = (1, 2, 3, 4, 5)
 SUMMED = {4: 0}
 ON_POOL = 6
 
@@ -46,6 +46,7 @@ def tile_selfattention_pa_kernel(tc, q_bytes, q_scale, k, out_0, out_1, out_2):
             return psum2.tile([P, 2, 512], F32, tag="banks", name=name)
 
         sct = const.tile([P, 2, 4], F32, name="sct")
+        sce = const.tile([P, D], F32, name="sce")
         qbytes = []
         kraw = []
         for i in range(4):
@@ -115,33 +116,42 @@ def tile_selfattention_pa_kernel(tc, q_bytes, q_scale, k, out_0, out_1, out_2):
         s1 = const.tile([P, NB], F32, name="s1")
         nm1s = const.tile([P, NB], F32, name="nm1s")
 
-        kc = const.tile([P, 2, T], U32, name="kc", align_bytes=64)
-        ks = const.tile([P, 2, T], U8, name="ks", align_bytes=64)
         KGROUPS = ((0, 4), (4, 2), (6, 2))
         gk = {}
+        kc = {}
+        ks = {}
         for b0, n in KGROUPS:
-            gkb = const.tile([P, 2, 512 * n], BF16, name="gk%d" % b0, align_bytes=64)
-            gk[b0] = gkb
-        qc = []
-        qs = []
-        for b in range(NB // 2):
-            qcb = const.tile([P, 512], U32, name="qc%d" % b, align_bytes=64)
-            qsb = const.tile([P, 512], U8, name="qs%d" % b, align_bytes=64)
-            qc.append(qcb)
-            qs.append(qsb)
+            gk[b0] = const.tile([P, 2, 512 * n], BF16, name="gk%d" % b0, align_bytes=64)
+            kc[b0] = const.tile([P, 2, P * n], U32, name="kc%d" % b0, align_bytes=64)
+            ks[b0] = const.tile([P, 2, P * n], U8, name="ks%d" % b0, align_bytes=64)
+
+        def group_of(b, groups):
+            return max(b0 for b0, n in groups if b0 <= b)
+        QGROUPS = ((0, 2), (2, 4), (6, 2))
+        qc = {}
+        qs = {}
+        for b0, n in QGROUPS:
+            qc[b0] = const.tile([P, 256 * n], U32, name="qc%d" % b0, align_bytes=64)
+            qs[b0] = const.tile([P, 256 * n], U8, name="qs%d" % b0, align_bytes=64)
 
         def transposes(src, bank):
             words = src.bitcast(F32)
             for g in range(2):
                 for u in range(2):
                     nc.tensor.transpose(
-                        bank[:, P * (2 * g + u) : P * (2 * g + u + 1)], words[:, 256 * g + u : 256 * (g + 1) : 2], ident[:]
+                        bank[:, P * (2 * u + g) : P * (2 * u + g + 1)], words[:, 256 * g + u : 256 * (g + 1) : 2], ident[:]
                     )
 
         gq = {}
 
-        def new_pair(i):
-            gq[i] = stage.tile([P, 2 * D], BF16, tag="late" if i >= 2 else "early", name="gq", align_bytes=64, bufs=1 if i >= 2 else 2)
+        def gq_of(b):
+            b0 = group_of(b, QGROUPS)
+            if b0 not in gq:
+                n = dict(QGROUPS)[b0]
+                gq[b0] = stage.tile(
+                    [P, n * D], BF16, tag="late" if b0 > 0 else "early", name="gq", align_bytes=64, bufs=1
+                )
+            return gq[b0][:, D * (b - b0) : D * (b - b0 + 1)]
 
         qbf = {}
         qbank = {}
@@ -163,38 +173,31 @@ def tile_selfattention_pa_kernel(tc, q_bytes, q_scale, k, out_0, out_1, out_2):
             qbank[b] = bank
 
         def scale_out(b):
-            if b % 2 == 0:
-                new_pair(b // 2)
-            for g in range(2):
-                lo = D * (b % 2) + 512 * g
-                nc.vector.tensor_tensor(
-                    out=gq[b // 2][:, lo : lo + 512].rearrange("p (r u e) -> p r u e", u=2, e=2),
-                    in0=qbank[b][:, 256 * g : 256 * (g + 1)].bitcast(BF16).rearrange("p (u r e) -> p r u e", u=2, e=2),
-                    in1=sct[:, g, :].rearrange("p (u e) -> p u e", u=2).unsqueeze(1).to_broadcast([P, P, 2, 2]),
-                    op=ALU.mult,
-                )
+            nc.vector.tensor_tensor(
+                out=gq_of(b).rearrange("p (c u e) -> p c u e", u=2, e=2),
+                in0=qbank[b].bitcast(BF16).rearrange("p (u c e) -> p c u e", u=2, e=2),
+                in1=sce[:].rearrange("p (c u e) -> p c u e", u=2, e=2),
+                op=ALU.mult,
+            )
 
         def copy_out(b):
             t = stage.tile([P, D], BF16, tag="graw", name="graw")
             nc.scalar.copy(
-                out=t[:].bitcast(F32).rearrange("p (g r u) -> p g r u", g=2, u=2),
-                in_=qbank[b].rearrange("p (g u r) -> p g r u", g=2, u=2),
+                out=t[:].bitcast(F32).rearrange("p (c u) -> p c u", u=2),
+                in_=qbank[b].rearrange("p (u c) -> p c u", u=2),
             )
             graw[b] = t
 
         def scale_pool(b):
-            if b % 2 == 0:
-                new_pair(b // 2)
-            lo = D * (b % 2)
             nc.gpsimd.tensor_tensor(
-                out=gq[b // 2][:, lo : lo + D].rearrange("p (g r t) -> p g r t", g=2, t=4),
+                out=gq_of(b).rearrange("p (g r t) -> p g r t", g=2, t=4),
                 in0=graw[b][:].rearrange("p (g r t) -> p g r t", g=2, t=4),
                 in1=sct[:].unsqueeze(2).to_broadcast([P, 2, P, 4]),
                 op=ALU.mult,
             )
 
-        def qq(pair):
-            nc.vector.quantize_mx(out=qc[pair][:].bitcast(FP8X4), scales=qs[pair][:], in_=gq[pair][:])
+        def qq(b0):
+            nc.vector.quantize_mx(out=qc[b0][:].bitcast(FP8X4), scales=qs[b0][:], in_=gq[b0][:])
 
         def k_turn(b):
             kbank[b] = two_banks("kturn")[:, 0, :] if True else one_bank("kturn")[:]
@@ -202,20 +205,19 @@ def tile_selfattention_pa_kernel(tc, q_bytes, q_scale, k, out_0, out_1, out_2):
 
         def k_copy(b):
             bank = kbank[b]
-            b0 = max(x for x, n in KGROUPS if x <= b)
+            b0 = group_of(b, KGROUPS)
             j = b - b0
             gw = gk[b0][:].rearrange("p g c -> p (g c)").bitcast(F32).rearrange("p (g r u) -> p g r u", g=2, u=2)
             nc.scalar.copy(
-                out=gw[:, :, P * j : P * (j + 1), :], in_=bank.rearrange("p (g u r) -> p g r u", g=2, u=2)
+                out=gw[:, :, P * j : P * (j + 1), :], in_=bank.rearrange("p (u g r) -> p g r u", g=2, u=2)
             )
 
-        def k_quant(b, n):
-            for g in range(2):
-                nc.vector.quantize_mx(
-                    out=kc[:, g, P * b : P * (b + n)].bitcast(FP8X4),
-                    scales=ks[:, g, P * b : P * (b + n)],
-                    in_=gk[b][:, g, :],
-                )
+        def k_quant(b0):
+            nc.vector.quantize_mx(
+                out=kc[b0][:].rearrange("p g c -> p (g c)").bitcast(FP8X4),
+                scales=ks[b0][:].rearrange("p g c -> p (g c)"),
+                in_=gk[b0][:].rearrange("p g c -> p (g c)"),
+            )
 
         def window(r):
             return max(0, P * r - 256), min(T, P * r + 384)
@@ -265,7 +267,10 @@ def tile_selfattention_pa_kernel(tc, q_bytes, q_scale, k, out_0, out_1, out_2):
             place = 0
             while place < len(blocks):
                 n = 1
-                while place + n < len(blocks) and blocks[place + n] == blocks[place] + n:
+                while (
+                    place + n < len(blocks) and blocks[place + n] == blocks[place] + n
+                    and group_of(blocks[place + n], KGROUPS) == group_of(blocks[place], KGROUPS)
+                ):
                     n += 1
                 if n == 3:
                     n = 2
@@ -278,13 +283,15 @@ def tile_selfattention_pa_kernel(tc, q_bytes, q_scale, k, out_0, out_1, out_2):
             logits[r] = acc
             for h in range(2):
                 for place, blk, n in runs_of(lays[r]["banks"][h]):
+                    k0, q0 = group_of(blk, KGROUPS), group_of(r, QGROUPS)
+                    key, row = P * (blk - k0), 256 * (r - q0)
                     for g in range(2):
                         nc.tensor.matmul_mx(
                             out=acc[:, h, P * place : P * (place + n)],
-                            lhsT=qc[r // 2][:, 256 * (r % 2) + P * g : 256 * (r % 2) + P * (g + 1)].bitcast(FP8X4),
-                            lhsT_scale=qs[r // 2][:, 256 * (r % 2) + P * g : 256 * (r % 2) + P * (g + 1)],
-                            rhs=kc[:, g, P * blk : P * (blk + n)].bitcast(FP8X4),
-                            rhs_scale=ks[:, g, P * blk : P * (blk + n)],
+                            lhsT=qc[q0][:, row + P * g : row + P * (g + 1)].bitcast(FP8X4),
+                            lhsT_scale=qs[q0][:, row + P * g : row + P * (g + 1)],
+                            rhs=kc[k0][:, g, key : key + P * n].bitcast(FP8X4),
+                            rhs_scale=ks[k0][:, g, key : key + P * n],
                             start=(g == 0),
                             stop=(g == 1),
                         )
@@ -436,12 +443,26 @@ def tile_selfattention_pa_kernel(tc, q_bytes, q_scale, k, out_0, out_1, out_2):
             junk = work.tile([P, T], F32, tag="junk", name="junk")
             nc.scalar.activation(out=junk[:], in_=st[r]["pr"][:], func=ACT.Copy, accum_out=s1[:, r : r + 1])
 
-        def prod_sum_vector(r):
-            pr = work.tile([P, T], F32, tag="pr", name="pr")
+        halves = const.tile([P, 2], F32, name="halves")
+
+        def prod_half(r):
+            pr = work.tile([P, 512], F32, tag="half", name="half")
+            nc.gpsimd.tensor_tensor(out=pr[:], in0=st[r]["e1"][:, 512:T], in1=row_part(r)[:, 512:T], op=ALU.mult)
+            st[r]["half"] = pr
+
+        def sum_half(r):
+            junk = work.tile([P, T], F32, tag="junk", name="junk")
+            nc.scalar.activation(out=junk[:, 0:512], in_=st[r]["half"][:], func=ACT.Copy, accum_out=halves[:, 1:2])
+
+        def prod_sum_vector(r, n, out):
+            scrap = work.tile([P, T], F32, tag="scrap", name="scrap")
             nc.vector.scalar_tensor_tensor(
-                out=pr[:], in0=row_part(r), scalar=1.0, in1=st[r]["e1"][:], op0=ALU.mult, op1=ALU.mult,
-                accum_out=s1[:, r : r + 1],
+                out=scrap[:, 0:n], in0=row_part(r)[:, 0:n], scalar=1.0, in1=st[r]["e1"][:, 0:n], op0=ALU.mult,
+                op1=ALU.mult, accum_out=out,
             )
+
+        def add_halves(r):
+            nc.vector.tensor_tensor(out=s1[:, r : r + 1], in0=halves[:, 0:1], in1=halves[:, 1:2], op=ALU.add)
 
         def pdiv(r):
             w = width_window(r)
@@ -472,13 +493,18 @@ def tile_selfattention_pa_kernel(tc, q_bytes, q_scale, k, out_0, out_1, out_2):
         rtot = const.tile([P, 1], F32, name="rtot")
         turned = {}
 
+        dsum = const.tile([P, 1], F32, name="dsum")
+
+        def sum_div():
+            nc.vector.tensor_reduce(out=dsum[:], in_=fin[:, 0:NB], axis=AX.X, op=ALU.add)
+
+        def total_div():
+            turned["tot"] = two_banks("tot")[:, 0, :]
+            nc.tensor.matmul(turned["tot"][:, 0:1], lhsT=ones[:], rhs=dsum[:], start=True, stop=True)
+
         def div_out():
-            tot = one_bank("tot")
-            for r in range(NB):
-                nc.tensor.matmul(tot[:, 0:1], lhsT=ones[:], rhs=fin[:, r : r + 1], start=(r == 0), stop=(r == last))
             turned[0] = two_banks("turned")[:, 0, :]
             nc.tensor.transpose(turned[0][:, 0:P], fin[:], ident[:])
-            turned["tot"] = tot
 
         def div_store():
             nc.vector.reciprocal(out=rtot[:], in_=turned["tot"][:, 0:1])
@@ -505,6 +531,9 @@ def tile_selfattention_pa_kernel(tc, q_bytes, q_scale, k, out_0, out_1, out_2):
         with tc.manual_schedule():
             cast(0, nc.vector)
             cast(1, nc.vector)
+            nc.vector.tensor_copy(
+                out=sce[:].rearrange("p (g r t) -> p g r t", g=2, t=4), in_=sct[:].unsqueeze(2).to_broadcast([P, 2, P, 4])
+            )
             cast(2, nc.scalar)
             turn(0)
             scale_out(0)
@@ -528,6 +557,7 @@ def tile_selfattention_pa_kernel(tc, q_bytes, q_scale, k, out_0, out_1, out_2):
             k_turn(3)
             k_copy(3)
             turn(5)
+            qq(0)
             scale_out(5)
             cast(6, nc.gpsimd)
             k_turn(4)
@@ -539,11 +569,9 @@ def tile_selfattention_pa_kernel(tc, q_bytes, q_scale, k, out_0, out_1, out_2):
             k_turn(7)
             k_copy(7)
             cast(7, nc.scalar)
-            qq(0)
-            k_quant(0, 4)
-            k_quant(4, 2)
-            k_quant(6, 2)
-            qq(1)
+            k_quant(0)
+            k_quant(4)
+            k_quant(6)
             qq(2)
             turn(6)
             copy_out(6)
@@ -581,7 +609,7 @@ def tile_selfattention_pa_kernel(tc, q_bytes, q_scale, k, out_0, out_1, out_2):
                     exp2(i)
                     exp1(i)
                 if i == 2:
-                    qq(3)
+                    qq(6)
                     prod_el(0)
                 if 1 <= i - 1 < ON_POOL:
                     prod_el(i - 1)
@@ -592,20 +620,26 @@ def tile_selfattention_pa_kernel(tc, q_bytes, q_scale, k, out_0, out_1, out_2):
                 if i >= 1:
                     rcp(i - 1)
             pdiv(last - 2)
-            norm(last - 1, True)
             rcp(last)
+            fold(last - 2)
+            prod_half(last - 1)
             log_z()
-            sum_el(last - 2)
             sum_fold(last - 3)
-            pdiv(last - 1)
+            sum_half(last - 1)
+            sum_fold(last - 2)
             norm(last, True)
-            prod_sum_vector(last - 1)
-            row_inverse()
-            prod_sum_vector(last)
-            row_log()
+            norm(last - 1, True)
             pdiv(last)
-            row_mean()
+            pdiv(last - 1)
+            prod_sum_vector(last - 1, 512, halves[:, 0:1])
+            sum_div()
+            total_div()
             div_out()
+            row_inverse()
+            prod_sum_vector(last, T, s1[:, last : last + 1])
+            row_log()
+            add_halves(last - 1)
+            row_mean()
             entropy_out()
             div_store()
             entropy_store()

import math
from contextlib import ExitStack

import concourse.mybir as mybir
from concourse.masks import make_identity

FLOPS = 2 * 1024 * 1024 * 1024

F32 = mybir.dt.float32
BF16 = mybir.dt.bfloat16
U32 = mybir.dt.uint32
U8 = mybir.dt.uint8
FP8 = mybir.dt.float8_e4m3fn
FP8X4 = mybir.dt.float8_e4m3fn_x4
ALU = mybir.AluOpType
ACT = mybir.ActivationFunctionType
AX = mybir.AxisListType

P = 128
T = 1024
D = 1024
NB = T // P
BAND = 250
WIN = 640
EDGE = 136
BIG = 2.0 ** 100
FOLDED = (1, 2, 3, 4, 5)
SUMMED = {4: 0}
ON_POOL = 6


def tile_selfattention_pa_kernel(tc, q_bytes, q_scale, k, out_0, out_1, out_2):
    nc = tc.nc
    with ExitStack() as ctx:
        const = ctx.enter_context(tc.tile_pool(name="const", bufs=1))
        stage = ctx.enter_context(tc.tile_pool(name="stage", bufs=4))
        work = ctx.enter_context(tc.tile_pool(name="work", bufs=4))
        small = ctx.enter_context(tc.tile_pool(name="small", bufs=4))
        psum = ctx.enter_context(tc.psum_pool(name="psum", bufs=2))
        psum2 = ctx.enter_context(tc.psum_pool(name="psum2", bufs=3))

        def one_bank(name):
            return psum.tile([P, 512], F32, tag="bank", name=name)

        def two_banks(name):
            return psum2.tile([P, 2, 512], F32, tag="banks", name=name)

        sct = const.tile([P, 2, 4], F32, name="sct")
        sce = const.tile([P, D], F32, name="sce")
        qbytes = []
        kraw = []
        for i in range(4):
            qb = const.tile([P, 2, D], U8, name="qbytes%d" % i)
            qbytes.append(qb)
        for b in range(NB):
            kr = const.tile([P, D], BF16, name="kraw%d" % b)
            kraw.append(kr)

        def load_q(b):
            nc.sync.dma_start(out=qbytes[b // 2][:, b % 2, :], in_=q_bytes[P * b : P * (b + 1), :])

        def load_q_pair(i):
            nc.sync.dma_start(
                out=qbytes[i][:], in_=q_bytes[256 * i : 256 * (i + 1), :].rearrange("(b p) k -> p b k", p=P)
            )

        def load_k(b):
            nc.sync.dma_start(out=kraw[b][:], in_=k[P * b : P * (b + 1), :])

        nc.scalar.dma_start(out=sct[:], in_=q_scale.rearrange("o (g p t) -> p (o g) t", p=P, t=4))
        load_q(0)
        load_q(1)
        load_q_pair(1)
        load_k(0)
        load_k(1)
        load_q_pair(2)
        load_k(2)
        load_k(3)
        load_q_pair(3)
        load_k(4)
        load_k(5)
        load_k(6)
        load_k(7)

        warm = const.tile([P, 1], F32, name="warm")
        warm2 = const.tile([P, 1], F32, name="warm2")
        nc.vector.memset(warm[:], 0.0)
        nc.scalar.activation(out=warm2[:], in_=warm[:], func=ACT.Exp)

        ident = const.tile([P, P], F32, name="ident")
        make_identity(nc, ident[:])
        zeros = const.tile([P, WIN], F32, name="zeros")
        mask = const.tile([P, 2 * EDGE + P], F32, name="mask")
        nc.vector.memset(mask[:], 0.0)
        nc.vector.memset(zeros[:], 0.0)
        nc.gpsimd.affine_select(
            out=mask[:, EDGE : 2 * EDGE], in_=mask[:, EDGE : 2 * EDGE], pattern=[[1, EDGE]], compare_op=ALU.is_ge, fill=BIG,
            base=-(256 - BAND + 1), channel_multiplier=-1,
        )
        nc.gpsimd.affine_select(
            out=mask[:, 0:EDGE], in_=mask[:, 0:EDGE], pattern=[[-1, EDGE]], compare_op=ALU.is_ge, fill=BIG,
            base=BAND - 1 - (WIN - 256 - EDGE), channel_multiplier=1,
        )
        nc.gpsimd.affine_select(
            out=mask[:, 2 * EDGE :], in_=mask[:, 2 * EDGE :], pattern=[[1, P]], compare_op=ALU.not_equal, fill=BIG,
            base=0, channel_multiplier=-1,
        )
        ones = const.tile([P, P], F32, name="ones")
        nc.vector.memset(ones[:], 1.0)
        fin = const.tile([P, P], F32, name="fin")
        nc.vector.memset(fin[:], 0.0)
        ent = const.tile([P, P], F32, name="ent")
        nc.vector.memset(ent[:], 0.0)

        z1 = const.tile([P, NB], F32, name="z1")
        s1 = const.tile([P, NB], F32, name="s1")
        nm1s = const.tile([P, NB], F32, name="nm1s")

        KGROUPS = ((0, 4), (4, 2), (6, 2))
        gk = {}
        kc = {}
        ks = {}
        for b0, n in KGROUPS:
            gk[b0] = const.tile([P, 2, 512 * n], BF16, name="gk%d" % b0, align_bytes=64)
            kc[b0] = const.tile([P, 2, P * n], U32, name="kc%d" % b0, align_bytes=64)
            ks[b0] = const.tile([P, 2, P * n], U8, name="ks%d" % b0, align_bytes=64)

        def group_of(b, groups):
            return max(b0 for b0, n in groups if b0 <= b)
        QGROUPS = ((0, 2), (2, 4), (6, 2))
        qc = {}
        qs = {}
        for b0, n in QGROUPS:
            qc[b0] = const.tile([P, 256 * n], U32, name="qc%d" % b0, align_bytes=64)
            qs[b0] = const.tile([P, 256 * n], U8, name="qs%d" % b0, align_bytes=64)

        def transposes(src, bank):
            words = src.bitcast(F32)
            for g in range(2):
                for u in range(2):
                    nc.tensor.transpose(
                        bank[:, P * (2 * u + g) : P * (2 * u + g + 1)], words[:, 256 * g + u : 256 * (g + 1) : 2], ident[:]
                    )

        gq = {}

        def gq_of(b):
            b0 = group_of(b, QGROUPS)
            if b0 not in gq:
                n = dict(QGROUPS)[b0]
                gq[b0] = stage.tile(
                    [P, n * D], BF16, tag="late" if b0 > 0 else "early", name="gq", align_bytes=64, bufs=1
                )
            return gq[b0][:, D * (b - b0) : D * (b - b0 + 1)]

        qbf = {}
        qbank = {}
        kbank = {}
        graw = {}

        def cast(b, engine):
            t = stage.tile([P, D], BF16, tag="qbf", name="qbf")
            src = qbytes[b // 2][:, b % 2, :].bitcast(FP8)
            if engine is nc.scalar:
                nc.scalar.copy(out=t[:], in_=src)
            else:
                engine.tensor_copy(out=t[:], in_=src)
            qbf[b] = t

        def turn(b):
            bank = two_banks("turn")[:, 0, :] if b == 2 else one_bank("turn")[:]
            transposes(qbf[b][:], bank)
            qbank[b] = bank

        def scale_out(b):
            nc.vector.tensor_tensor(
                out=gq_of(b).rearrange("p (c u e) -> p c u e", u=2, e=2),
                in0=qbank[b].bitcast(BF16).rearrange("p (u c e) -> p c u e", u=2, e=2),
                in1=sce[:].rearrange("p (c u e) -> p c u e", u=2, e=2),
                op=ALU.mult,
            )

        def copy_out(b):
            t = stage.tile([P, D], BF16, tag="graw", name="graw")
            nc.scalar.copy(
                out=t[:].bitcast(F32).rearrange("p (c u) -> p c u", u=2),
                in_=qbank[b].rearrange("p (u c) -> p c u", u=2),
            )
            graw[b] = t

        def scale_pool(b):
            nc.gpsimd.tensor_tensor(
                out=gq_of(b).rearrange("p (g r t) -> p g r t", g=2, t=4),
                in0=graw[b][:].rearrange("p (g r t) -> p g r t", g=2, t=4),
                in1=sct[:].unsqueeze(2).to_broadcast([P, 2, P, 4]),
                op=ALU.mult,
            )

        def qq(b0):
            nc.vector.quantize_mx(out=qc[b0][:].bitcast(FP8X4), scales=qs[b0][:], in_=gq[b0][:])

        def k_turn(b):
            kbank[b] = two_banks("kturn")[:, 0, :] if True else one_bank("kturn")[:]
            transposes(kraw[b][:], kbank[b])

        def k_copy(b):
            bank = kbank[b]
            b0 = group_of(b, KGROUPS)
            j = b - b0
            gw = gk[b0][:].rearrange("p g c -> p (g c)").bitcast(F32).rearrange("p (g r u) -> p g r u", g=2, u=2)
            nc.scalar.copy(
                out=gw[:, :, P * j : P * (j + 1), :], in_=bank.rearrange("p (u g r) -> p g r u", g=2, u=2)
            )

        def k_quant(b0):
            nc.vector.quantize_mx(
                out=kc[b0][:].rearrange("p g c -> p (g c)").bitcast(FP8X4),
                scales=ks[b0][:].rearrange("p g c -> p (g c)"),
                in_=gk[b0][:].rearrange("p g c -> p (g c)"),
            )

        def window(r):
            return max(0, P * r - 256), min(T, P * r + 384)

        def zero_fill(r):
            c0, c1 = window(r)
            if c0 > 0:
                nc.sync.dma_start(out=out_0[P * r : P * (r + 1), 0:c0], in_=zeros[:, 0:c0])
            if c1 < T:
                nc.sync.dma_start(out=out_0[P * r : P * (r + 1), c1:T], in_=zeros[:, 0 : T - c1])

        CORE = P - (EDGE - P)

        def layout(r):
            want = [r + 1, r + 2, r - 2, r - 1]
            far = [x for x in range(NB) if x != r and x not in want]
            first = []
            for x in want:
                first.append(x if 0 <= x < NB else far.pop(0))
            lay = {"banks": [first, [r] + far]}
            base = P * r - 256
            right = WIN - EDGE
            edges = []
            if r + 1 < NB:
                edges.append((CORE, 0, base + right, EDGE if r + 2 < NB else EDGE - P))
            if r > 0:
                if r > 1:
                    edges.append((256, EDGE, base, EDGE))
                else:
                    edges.append((384, EDGE + P, 0, EDGE - P))
            lay["edges"] = edges
            core = []
            if r + 1 < NB:
                core.append((0, P * (r + 1)))
            if r > 0:
                core.append((512 - CORE, base + EDGE))
            lay["core"] = core
            lay["rest"] = (CORE if r + 1 < NB else 0, 512 - CORE if r > 0 else 512)
            return lay

        lays = [layout(r) for r in range(NB)]
        logits = {}
        st = {}

        def runs_of(blocks):
            out = []
            place = 0
            while place < len(blocks):
                n = 1
                while (
                    place + n < len(blocks) and blocks[place + n] == blocks[place] + n
                    and group_of(blocks[place + n], KGROUPS) == group_of(blocks[place], KGROUPS)
                ):
                    n += 1
                if n == 3:
                    n = 2
                out.append((place, blocks[place], n))
                place += n
            return out

        def mm(r):
            acc = two_banks("acc")
            logits[r] = acc
            for h in range(2):
                for place, blk, n in runs_of(lays[r]["banks"][h]):
                    k0, q0 = group_of(blk, KGROUPS), group_of(r, QGROUPS)
                    key, row = P * (blk - k0), 256 * (r - q0)
                    for g in range(2):
                        nc.tensor.matmul_mx(
                            out=acc[:, h, P * place : P * (place + n)],
                            lhsT=qc[q0][:, row + P * g : row + P * (g + 1)].bitcast(FP8X4),
                            lhsT_scale=qs[q0][:, row + P * g : row + P * (g + 1)],
                            rhs=kc[k0][:, g, key : key + P * n].bitcast(FP8X4),
                            rhs_scale=ks[k0][:, g, key : key + P * n],
                            start=(g == 0),
                            stop=(g == 1),
                        )

        def width_masked(r):
            return P + sum(e[3] for e in lays[r]["edges"])

        def width_core(r):
            return CORE * len(lays[r]["core"])

        def a_core(r):
            work_w = work.tile([P, 1 + 400 + T], F32, tag="w", name="w")
            st[r] = {"lead": work_w, "w": work_w[:, 1:]}
            m = width_masked(r)
            core = lays[r]["core"]
            out = st[r]["w"][:, m : m + CORE * len(core)]
            if len(core) == 2:
                step = 512 - CORE
                flat = logits[r][:].rearrange("p b c -> p (b c)")
                src = flat[:, 0 : 2 * step].rearrange("p (a c) -> p a c", c=step)[:, :, 0:CORE]
                out = out.rearrange("p (a c) -> p a c", a=2)
            else:
                src = logits[r][:, 0, core[0][0] : core[0][0] + CORE]
            nc.vector.tensor_scalar(
                out=out, in0=src, scalar1=-1.0, scalar2=None, op0=ALU.mult, op1=ALU.min,
                accum_out=work_w[:, 0:1],
            )

        def a_rest(r):
            t1 = small.tile([P, 1], F32, tag="t1", name="t1")
            st[r]["t1"] = t1
            lo, hi = lays[r]["rest"]
            at = width_masked(r) + width_core(r)
            nc.vector.tensor_scalar(
                out=st[r]["w"][:, at : at + hi - lo], in0=logits[r][:, 0, lo:hi], scalar1=-1.0,
                scalar2=st[r]["lead"][:, 0:1], op0=ALU.mult, op1=ALU.min, accum_out=t1[:],
            )

        def a_second(r):
            lo = width_masked(r) + 512
            nc.vector.tensor_scalar(
                out=st[r]["w"][:, lo : lo + 512], in0=logits[r][:, 1, :], scalar1=-1.0, scalar2=st[r]["t1"][:],
                op0=ALU.mult, op1=ALU.min, accum_out=nm1s[:, r : r + 1],
            )

        def mask_edges(r):
            runs = []
            for s, ms, key, w in lays[r]["edges"]:
                if runs and runs[-1][0] + runs[-1][2] == s and runs[-1][1] + runs[-1][2] == ms:
                    runs[-1][2] += w
                else:
                    runs.append([s, ms, w])
            at = 0
            for s, ms, w in runs:
                nc.vector.tensor_tensor(
                    out=st[r]["w"][:, at : at + w], in0=mask[:, ms : ms + w], in1=logits[r][:, 0, s : s + w],
                    op=ALU.subtract,
                )
                at += w

        def mask_diag(r):
            m = width_masked(r)
            nc.vector.tensor_tensor(
                out=st[r]["w"][:, m - P : m], in0=mask[:, 2 * EDGE :], in1=logits[r][:, 1, 0:P], op=ALU.subtract
            )

        def min_masked(r):
            m = width_masked(r)
            nm2 = small.tile([P, 1], F32, tag="nm2", name="nm2")
            nc.vector.tensor_reduce(out=nm2[:], in_=st[r]["lead"][:, 0 : 1 + m], axis=AX.X, op=ALU.min)
            st[r]["nm2"] = nm2

        def width_window(r):
            return width_masked(r) + width_core(r)

        def row_part(r):
            m = width_masked(r)
            return st[r]["w"][:, m : m + T]

        def exp1(r):
            e1 = work.tile([P, T], F32, tag="e1", name="e1")
            nc.scalar.activation(
                out=e1[:], in_=row_part(r), func=ACT.Exp, bias=nm1s[:, r : r + 1], scale=-1.0,
                accum_out=z1[:, r : r + 1],
            )
            st[r]["e1"] = e1

        def exp2(r):
            w = width_window(r)
            e2 = work.tile([P, WIN], F32, tag="e2", name="e2")
            z2 = small.tile([P, 1], F32, tag="z2", name="z2")
            nc.scalar.activation(
                out=e2[:, 0:w], in_=st[r]["w"][:, 0:w], func=ACT.Exp, bias=st[r]["nm2"][:], scale=-1.0, accum_out=z2[:]
            )
            st[r]["e2"] = e2
            st[r]["z2"] = z2

        def rcp(r):
            rz2 = small.tile([P, 1], F32, tag="rz2", name="rz2")
            nc.vector.reciprocal(out=rz2[:], in_=st[r]["z2"][:])
            st[r]["rz2"] = rz2

        def norm(r, on_vector):
            w = width_window(r)
            att = work.tile([P, WIN], F32, tag="att", name="att")
            if on_vector:
                nc.vector.tensor_scalar(
                    out=att[:, 0:w], in0=st[r]["e2"][:, 0:w], scalar1=st[r]["rz2"][:], scalar2=None, op0=ALU.mult
                )
            else:
                nc.scalar.activation(out=att[:, 0:w], in_=st[r]["e2"][:, 0:w], func=ACT.Copy, scale=st[r]["rz2"][:])
            st[r]["att"] = att
            store_att(r)

        def store_att(r):
            att = st[r]["att"]
            rows = slice(P * r, P * (r + 1))
            at = 0
            for s, ms, key, w in lays[r]["edges"]:
                nc.sync.dma_start(out=out_0[rows, key : key + w], in_=att[:, at : at + w])
                at += w
            nc.sync.dma_start(out=out_0[rows, P * r : P * (r + 1)], in_=att[:, at : at + P])
            at += P
            for start, key in lays[r]["core"]:
                nc.sync.dma_start(out=out_0[rows, key : key + CORE], in_=att[:, at : at + CORE])
                at += CORE

        def prod_el(r):
            if r == 0:
                pr = stage.tile([P, T], F32, tag="late", name="pr", align_bytes=64, bufs=1)
            else:
                pr = work.tile([P, T], F32, tag="pr", name="pr")
            nc.gpsimd.tensor_tensor(out=pr[:], in0=st[r]["e1"][:], in1=row_part(r), op=ALU.mult)
            st[r]["pr"] = pr

        def fold(r):
            acc = one_bank("fold")
            for b in range(NB):
                nc.tensor.matmul(
                    acc[:, 0:P], lhsT=ident[:], rhs=st[r]["pr"][:, P * b : P * (b + 1)], start=(b == 0), stop=(b == NB - 1)
                )
            st[r]["fold"] = acc

        def sum_fold(r):
            junk = work.tile([P, T], F32, tag="junk", name="junk")
            nc.scalar.activation(out=junk[:, 0:P], in_=st[r]["fold"][:, 0:P], func=ACT.Copy, accum_out=s1[:, r : r + 1])

        def sum_el(r):
            junk = work.tile([P, T], F32, tag="junk", name="junk")
            nc.scalar.activation(out=junk[:], in_=st[r]["pr"][:], func=ACT.Copy, accum_out=s1[:, r : r + 1])

        halves = const.tile([P, 2], F32, name="halves")

        def prod_half(r):
            pr = work.tile([P, 512], F32, tag="half", name="half")
            nc.gpsimd.tensor_tensor(out=pr[:], in0=st[r]["e1"][:, 512:T], in1=row_part(r)[:, 512:T], op=ALU.mult)
            st[r]["half"] = pr

        def sum_half(r):
            junk = work.tile([P, T], F32, tag="junk", name="junk")
            nc.scalar.activation(out=junk[:, 0:512], in_=st[r]["half"][:], func=ACT.Copy, accum_out=halves[:, 1:2])

        def prod_sum_vector(r, n, out):
            scrap = work.tile([P, T], F32, tag="scrap", name="scrap")
            nc.vector.scalar_tensor_tensor(
                out=scrap[:, 0:n], in0=row_part(r)[:, 0:n], scalar=1.0, in1=st[r]["e1"][:, 0:n], op0=ALU.mult,
                op1=ALU.mult, accum_out=out,
            )

        def add_halves(r):
            nc.vector.tensor_tensor(out=s1[:, r : r + 1], in0=halves[:, 0:1], in1=halves[:, 1:2], op=ALU.add)

        def pdiv(r):
            w = width_window(r)
            junk2 = work.tile([P, WIN], F32, tag="junk2", name="junk2")
            nc.vector.tensor_scalar(
                out=junk2[:, 0:w], in0=st[r]["att"][:, 0:w], scalar1=1.0, scalar2=None,
                op0=ALU.subtract, op1=ALU.mult, accum_out=fin[:, r : r + 1],
            )

        lnz = const.tile([P, NB], F32, name="lnz")

        def log_z():
            nc.scalar.activation(out=lnz[:], in_=z1[:], func=ACT.Ln)

        shifted = const.tile([P, NB], F32, name="shifted")
        rz1 = const.tile([P, NB], F32, name="rz1")
        mean = const.tile([P, NB], F32, name="mean")

        def row_log():
            nc.vector.tensor_tensor(out=shifted[:], in0=lnz[:], in1=nm1s[:], op=ALU.subtract)

        def row_inverse():
            nc.vector.reciprocal(out=rz1[:], in_=z1[:])

        def row_mean():
            nc.vector.tensor_tensor(out=mean[:], in0=s1[:], in1=rz1[:], op=ALU.mult)

        rtot = const.tile([P, 1], F32, name="rtot")
        turned = {}

        dsum = const.tile([P, 1], F32, name="dsum")

        def sum_div():
            nc.vector.tensor_reduce(out=dsum[:], in_=fin[:, 0:NB], axis=AX.X, op=ALU.add)

        def total_div():
            turned["tot"] = two_banks("tot")[:, 0, :]
            nc.tensor.matmul(turned["tot"][:, 0:1], lhsT=ones[:], rhs=dsum[:], start=True, stop=True)

        def div_out():
            turned[0] = two_banks("turned")[:, 0, :]
            nc.tensor.transpose(turned[0][:, 0:P], fin[:], ident[:])

        def div_store():
            nc.vector.reciprocal(out=rtot[:], in_=turned["tot"][:, 0:1])
            res = const.tile([NB, P], F32, name="res")
            nc.vector.tensor_scalar(
                out=res[:], in0=turned[0][0:NB, 0:P], scalar1=rtot[0:NB, :], scalar2=None, op0=ALU.mult
            )
            nc.sync.dma_start(out=out_2.rearrange("(r p) -> r p", p=P), in_=res[:])

        def entropy_out():
            nc.vector.tensor_tensor(out=ent[:, 0:NB], in0=mean[:], in1=shifted[:], op=ALU.add)
            turned2 = one_bank("turned2")
            nc.tensor.transpose(turned2[:, 0:P], ent[:], ident[:])
            turned[1] = turned2

        def entropy_store():
            res2 = const.tile([NB, P], F32, name="res2")
            nc.scalar.activation(
                out=res2[:], in_=turned[1][0:NB, 0:P], func=ACT.Copy, scale=1.0 / math.log(float(T)),
            )
            nc.sync.dma_start(out=out_1.rearrange("(r p) -> r p", p=P), in_=res2[:])

        last = NB - 1
        with tc.manual_schedule():
            cast(0, nc.vector)
            cast(1, nc.vector)
            nc.vector.tensor_copy(
                out=sce[:].rearrange("p (g r t) -> p g r t", g=2, t=4), in_=sct[:].unsqueeze(2).to_broadcast([P, 2, P, 4])
            )
            cast(2, nc.scalar)
            turn(0)
            scale_out(0)
            turn(1)
            scale_out(1)
            cast(3, nc.scalar)
            turn(2)
            scale_out(2)
            k_turn(0)
            k_copy(0)
            turn(3)
            scale_out(3)
            cast(4, nc.gpsimd)
            k_turn(1)
            k_copy(1)
            turn(4)
            scale_out(4)
            k_turn(2)
            k_copy(2)
            cast(5, nc.gpsimd)
            k_turn(3)
            k_copy(3)
            turn(5)
            qq(0)
            scale_out(5)
            cast(6, nc.gpsimd)
            k_turn(4)
            k_copy(4)
            k_turn(5)
            k_copy(5)
            k_turn(6)
            k_copy(6)
            k_turn(7)
            k_copy(7)
            cast(7, nc.scalar)
            k_quant(0)
            k_quant(4)
            k_quant(6)
            qq(2)
            turn(6)
            copy_out(6)
            mm(0)
            scale_pool(6)
            turn(7)
            copy_out(7)
            scale_pool(7)
            mm(1)
            for i in range(NB):
                if i + 2 < NB:
                    mm(i + 2)
                if i - 3 in FOLDED:
                    fold(i - 3)
                if i >= 1:
                    exp2(i - 1)
                if i >= 2:
                    norm(i - 2, False)
                if i == 2:
                    zero_fill(0)
                    zero_fill(1)
                if i >= 2:
                    zero_fill(i)
                a_core(i)
                mask_edges(i)
                if i >= 3:
                    pdiv(i - 3)
                a_rest(i)
                mask_diag(i)
                a_second(i)
                if i < last:
                    exp1(i)
                min_masked(i)
                if i == last:
                    exp2(i)
                    exp1(i)
                if i == 2:
                    qq(6)
                    prod_el(0)
                if 1 <= i - 1 < ON_POOL:
                    prod_el(i - 1)
                if i - 4 in FOLDED:
                    sum_fold(i - 4)
                if i in SUMMED:
                    sum_el(SUMMED[i])
                if i >= 1:
                    rcp(i - 1)
            pdiv(last - 2)
            rcp(last)
            fold(last - 2)
            prod_half(last - 1)
            log_z()
            sum_fold(last - 3)
            sum_half(last - 1)
            sum_fold(last - 2)
            norm(last, True)
            norm(last - 1, True)
            pdiv(last)
            pdiv(last - 1)
            prod_sum_vector(last - 1, 512, halves[:, 0:1])
            sum_div()
            total_div()
            div_out()
            row_inverse()
            prod_sum_vector(last, T, s1[:, last : last + 1])
            row_log()
            add_halves(last - 1)
            row_mean()
            entropy_out()
            div_store()
            entropy_store()
